import numpy as np
import ml_dtypes


def mxq(x, axis, fmt="e4m3"):
    dtype, down = {"e4m3": (ml_dtypes.float8_e4m3fn, 7), "e5m2": (ml_dtypes.float8_e5m2, 14)}[fmt]
    v = np.moveaxis(np.asarray(x, np.float32).astype(ml_dtypes.bfloat16).astype(np.float64), axis, -1)
    blocks = v.reshape(v.shape[:-1] + (-1, 32))
    amax = np.abs(blocks).max(-1, keepdims=True)
    byte = np.maximum(np.where(amax > 0, np.frexp(amax)[1] - 1 + 127, 0) - down, 1)
    scale = np.exp2(byte - 127.0)
    codes = (blocks / scale).astype(np.float32).astype(dtype).astype(np.float64)
    return np.moveaxis((codes * scale).reshape(v.shape), -1, axis)


WIDE = False


def mx_kscale(k):
    if not WIDE:
        return np.ones(k)
    levels = np.array([10, -10, 5, -5, 0])
    a = np.random.permutation(np.resize(levels, k // 512 * 4)).reshape(k // 512, 4)
    idx = np.arange(k)
    return np.exp2(a[idx // 512, idx % 128 // 32])


BF16 = ml_dtypes.bfloat16


def bf(x):
    return np.asarray(x, np.float32).astype(BF16)


def f64(x):
    return np.asarray(x).astype(np.float64)


B, N, D, DO, H, HID = 12, 128, 512, 512, 8, 2048
EPS = 1e-5


def gelu_tanh(v):
    return 0.5 * v * (1.0 + np.tanh(np.sqrt(2.0 / np.pi) * (v + 0.044715 * v**3)))


def layer_norm(v, g, b):
    m = v.mean(-1, keepdims=True)
    var = v.var(-1, keepdims=True)
    return (v - m) * (1.0 / np.sqrt(var + EPS)) * g + b


def setup_inputs():
    t = mx_kscale(D)
    return {
        "x": bf(np.random.standard_normal((B, N, D))),
        "h2": bf(np.random.standard_normal((B, N, D)) * 0.7),
        "xfeat_w": bf(np.random.standard_normal((D, D)) / np.sqrt(D)),
        "xfeat_b": bf(np.random.standard_normal(D) * 0.1),
        "pos_mix": bf(np.random.standard_normal((N, N)) * 0.5 / np.sqrt(N)),
        "ln2_g": bf((1.0 + 0.1 * np.random.standard_normal(D)) * t),
        "ln2_b": bf(0.1 * np.random.standard_normal(D) * t),
        "mlp_w1": bf(np.random.standard_normal((D, HID)) / np.sqrt(D) / t[:, None]),
        "mlp_b1": bf(0.1 * np.random.standard_normal(HID)),
    }


def reference(x, h2, xfeat_w, xfeat_b, pos_mix, ln2_g, ln2_b, mlp_w1, mlp_b1):
    xf = (mxq(f64(h2), 2, "e4m3") @ mxq(f64(xfeat_w), 0, "e4m3")) + f64(xfeat_b) + f64(pos_mix) @ f64(h2)
    x1 = f64(x) + xf
    h = layer_norm(x1, f64(ln2_g), f64(ln2_b))
    return gelu_tanh((mxq(h, 2, "e4m3") @ mxq(f64(mlp_w1), 0, "e4m3")) + f64(mlp_b1))

@@ -1,0 +1,352 @@
+from contextlib import ExitStack
+
+import concourse.mybir as mybir
+from concourse.masks import make_identity
+
+F32 = mybir.dt.float32
+BF16 = mybir.dt.bfloat16
+U32 = mybir.dt.uint32
+U8 = mybir.dt.uint8
+FP8X4 = mybir.dt.float8_e4m3fn_x4
+ACT = mybir.ActivationFunctionType
+ALU = mybir.AluOpType
+
+P = 128
+PACK = 4
+B = 12
+D = 512
+HID = 2048
+BANK = 512
+N_BLOCKS = HID // BANK
+GROUP = 4
+N_GROUPS = B // GROUP
+TOK = GROUP * P
+HALF = HID // 2
+EPS = 1e-5
+
+FLOPS = 2 * B * P * (D * D + D * HID + P * D)
+
+
+def runs_of_four(planes, grouped):
+    return (
+        grouped.rearrange("p (c i) t -> p c t i", i=4),
+        planes.rearrange("p t (c i) -> p c t i", i=4),
+    )
+
+
+def tile_gatblock_pb_kernel(
+    tc, x, h2, xfeat_w, xfeat_b, pos_mix, ln2_g, ln2_b, mlp_w1, mlp_b1, out
+):
+    nc = tc.nc
+    with ExitStack() as stack:
+        const = stack.enter_context(tc.tile_pool(name="const", bufs=1))
+        work = stack.enter_context(tc.tile_pool(name="work", bufs=2))
+        psum_tp = stack.enter_context(tc.psum_pool(name="psum_tp", bufs=2))
+        psum_t = stack.enter_context(tc.psum_pool(name="psum_t", bufs=2))
+        psum_y = stack.enter_context(tc.psum_pool(name="psum_y", bufs=1))
+        psum_o = stack.enter_context(tc.psum_pool(name="psum_o", bufs=3))
+        stack.enter_context(tc.manual_schedule())
+
+        h2_sb = [const.tile([P, GROUP, D], BF16, name="h2_sb%d" % g) for g in range(N_GROUPS)]
+        x_sb = [const.tile([P, GROUP, D], BF16, name="x_sb%d" % g) for g in range(N_GROUPS)]
+
+        def load_group(dst, src, g):
+            nc.sync.dma_start(
+                out=dst[g][:], in_=src[g * GROUP : (g + 1) * GROUP].rearrange("b n d -> n b d")
+            )
+
+        gb_rows = const.tile([P, P], BF16)
+        nc.vector.memset(gb_rows[:], 0.0)
+
+        load_group(h2_sb, h2, 0)
+        wx_planes = const.tile([P, PACK, D], BF16)
+        for u in range(2):
+            nc.sync.dma_start(
+                out=wx_planes[:, 2 * u : 2 * u + 2, :],
+                in_=xfeat_w[256 * u : 256 * (u + 1), :].rearrange("(q e) c -> q e c", e=2),
+            )
+        pos_sb = const.tile([P, P], BF16)
+        nc.sync.dma_start(out=pos_sb[:], in_=pos_mix)
+        load_group(x_sb, x, 0)
+        xfb_bc = const.tile([P, D], BF16)
+        nc.sync.dma_start(out=xfb_bc[:], in_=xfeat_b.partition_broadcast(P))
+        nc.sync.dma_start(out=gb_rows[0:PACK, :], in_=ln2_g.rearrange("(t p) -> t p", p=P))
+        nc.sync.dma_start(out=gb_rows[PACK : 2 * PACK, :], in_=ln2_b.rearrange("(t p) -> t p", p=P))
+        load_group(h2_sb, h2, 1)
+        load_group(h2_sb, h2, 2)
+        load_group(x_sb, x, 1)
+        w1_planes = []
+        for j in range(N_BLOCKS):
+            w1p = const.tile([P, PACK, BANK], BF16, name="w1_planes%d" % j)
+            nc.sync.dma_start(
+                out=w1p[:],
+                in_=mlp_w1[:, j * BANK : (j + 1) * BANK].rearrange("(t p) n -> p t n", p=P),
+            )
+            w1_planes.append(w1p)
+        load_group(x_sb, x, 2)
+        b1_bc = const.tile([P, HID], BF16)
+        nc.sync.dma_start(out=b1_bc[:], in_=mlp_b1.partition_broadcast(P))
+
+        warm = const.tile([P, 1], F32)
+        nc.vector.memset(warm[:], 0.0)
+        nc.scalar.activation(out=warm[:], in_=warm[:], func=ACT.Gelu_apprx_tanh)
+        neg_half = const.tile([P, GROUP], F32)
+        nc.vector.memset(neg_half[:], -0.5)
+        ident_f = const.tile([P, P], F32)
+        make_identity(nc, ident_f[:])
+        ident_b = const.tile([P, P], BF16)
+        make_identity(nc, ident_b[:])
+
+        row_sum = [const.tile([P, GROUP], F32, name="row_sum%d" % g) for g in range(N_GROUPS)]
+        neg_mean = [const.tile([P, GROUP], F32, name="neg_mean%d" % g) for g in range(N_GROUPS)]
+        sq_sum = [const.tile([P, GROUP], F32, name="sq_sum%d" % g) for g in range(N_GROUPS)]
+        var_eps = [const.tile([P, GROUP], F32, name="var_eps%d" % g) for g in range(N_GROUPS)]
+        rstd = [const.tile([P, GROUP], F32, name="rstd%d" % g) for g in range(N_GROUPS)]
+
+        wx_grouped = const.tile([P, D, PACK], BF16, align_bytes=64)
+        wx_codes = const.tile([P, D], U32, align_bytes=64)
+        wx_scales = const.tile([P, D], U8, align_bytes=64)
+        w1_codes = const.tile([P, HID], U32, align_bytes=64)
+        w1_scales = const.tile([P, HID], U8, align_bytes=64)
+        w1_grouped = [None] * N_BLOCKS
+        h2_grouped = [None] * N_GROUPS
+        h2_codes = [None] * N_GROUPS
+        h2_scales = [None] * N_GROUPS
+        h_planes = [None] * N_GROUPS
+        h_grouped = [None] * N_GROUPS
+        h_codes = [None] * N_GROUPS
+        h_scales = [None] * N_GROUPS
+        t_sb = [None] * B
+        x1 = [None] * B
+        normed = [None] * B
+        act = [None] * B
+
+        def transpose_h2(g):
+            h2_words = h2_sb[g][:].rearrange("p b d -> p (b d)").bitcast(F32)
+            h2_grouped[g] = work.tile([P, TOK * PACK], BF16, align_bytes=64, tag="h2g", name="h2g%d" % g)
+            grouped_words = h2_grouped[g][:].bitcast(F32).rearrange("p (n u) -> p n u", u=2)
+            for half in range(2):
+                h2T_ps = psum_tp.tile([P, 2, 2 * P], F32, tag="tp")
+                for s2 in range(2):
+                    for u in range(2):
+                        first = (2 * half + s2) * (D // 2) + u * P
+                        nc.tensor.transpose(
+                            h2T_ps[:, u, s2 * P : (s2 + 1) * P],
+                            h2_words[:, first : first + P],
+                            ident_f[:],
+                        )
+                nc.scalar.copy(
+                    out=grouped_words[:, half * 2 * P : (half + 1) * 2 * P, :],
+                    in_=h2T_ps[:].rearrange("p u n -> p n u"),
+                )
+
+        def quantise_h2(g):
+            h2_codes[g] = work.tile([P, TOK], U32, align_bytes=64, tag="h2c", name="h2c%d" % g)
+            h2_scales[g] = work.tile([P, TOK], U8, align_bytes=64, tag="h2s", name="h2s%d" % g)
+            nc.vector.quantize_mx(
+                out=h2_codes[g][:].bitcast(FP8X4), scales=h2_scales[g][:], in_=h2_grouped[g][:]
+            )
+
+        def plain_part(i):
+            g, s = divmod(i, GROUP)
+            t_ps = psum_t.tile([P, D], F32, tag="t")
+            nc.tensor.matmul(t_ps[:], lhsT=posT[:], rhs=h2_sb[g][:, s, :], start=True, stop=False)
+            nc.tensor.matmul(t_ps[:], lhsT=ident_b[:], rhs=x_sb[g][:, s, :], start=False, stop=True)
+            t_sb[i] = work.tile([P, D], F32, tag="t_sb", bufs=3, name="t_sb%d" % i)
+            nc.vector.tensor_tensor(out=t_sb[i][:], in0=t_ps[:], in1=xfb_bc[:], op=ALU.add)
+
+        def mx_part(i):
+            g, s = divmod(i, GROUP)
+            toks = slice(s * P, (s + 1) * P)
+            y_ps = psum_y.tile([P, D], F32, tag="y")
+            nc.tensor.matmul_mx(
+                out=y_ps[:],
+                lhsT=h2_codes[g][:, toks].bitcast(FP8X4),
+                lhsT_scale=h2_scales[g][:, toks],
+                rhs=wx_codes[:].bitcast(FP8X4),
+                rhs_scale=wx_scales[:],
+                start=True,
+                stop=True,
+            )
+            x1[i] = work.tile([P, D], F32, tag="x1", bufs=2 * GROUP, name="x1_%d" % i)
+            nc.vector.scalar_tensor_tensor(
+                out=x1[i][:],
+                in0=y_ps[:],
+                scalar=1.0,
+                in1=t_sb[i][:],
+                op0=ALU.mult,
+                op1=ALU.add,
+                accum_out=row_sum[g][:, s : s + 1],
+            )
+
+        def centred_squares(i):
+            g, s = divmod(i, GROUP)
+            col = slice(s, s + 1)
+            squares = work.tile([P, D], BF16, tag="squares", bufs=GROUP)
+            nc.scalar.activation(
+                out=squares[:],
+                in_=x1[i][:],
+                func=ACT.Square,
+                bias=row_sum[g][:, col],
+                scale=-1.0 * D,
+                accum_out=sq_sum[g][:, col],
+            )
+
+        def normalise(g):
+            nc.gpsimd.tensor_scalar(
+                out=neg_mean[g][:], in0=row_sum[g][:], scalar1=-1.0 / D, scalar2=0.0, op0=ALU.mult, op1=ALU.add
+            )
+            nc.gpsimd.tensor_scalar(
+                out=var_eps[g][:], in0=sq_sum[g][:], scalar1=1.0 / (D * D * D), scalar2=EPS, op0=ALU.mult, op1=ALU.add
+            )
+            nc.gpsimd.tensor_tensor(out=rstd[g][:], in0=var_eps[g][:], in1=neg_half[:], op=ALU.pow)
+            for s in range(GROUP):
+                i = g * GROUP + s
+                normed[i] = work.tile([P, D], F32, tag="normed", bufs=2 * GROUP, name="normed%d" % i)
+                nc.gpsimd.tensor_scalar(
+                    out=normed[i][:],
+                    in0=x1[i][:],
+                    scalar1=neg_mean[g][:, s : s + 1],
+                    scalar2=rstd[g][:, s : s + 1],
+                    op0=ALU.add,
+                    op1=ALU.mult,
+                )
+
+        def h_plane(g, t):
+            if t == 0:
+                h_planes[g] = work.tile([P, PACK, TOK], BF16, tag="h_planes", name="h_planes%d" % g)
+            nT_ps = psum_tp.tile([P, TOK], F32, tag="tp")
+            for s in range(GROUP):
+                nc.tensor.transpose(
+                    nT_ps[:, s * P : (s + 1) * P], normed[g * GROUP + s][:, t * P : (t + 1) * P], ident_f[:]
+                )
+            nc.scalar.activation(
+                out=h_planes[g][:, t, :],
+                in_=nT_ps[:],
+                func=ACT.Identity,
+                scale=gb[:, t : t + 1],
+                bias=gb[:, PACK + t : PACK + t + 1],
+            )
+
+        def regroup_h(g):
+            h_grouped[g] = work.tile([P, TOK, PACK], BF16, align_bytes=64, tag="h_grouped", name="h_grouped%d" % g)
+            nc.gpsimd.tensor_scalar(
+                out=h_grouped[g][:],
+                in0=h_planes[g][:].rearrange("p t c -> p c t"),
+                scalar1=1.0,
+                scalar2=0.0,
+                op0=ALU.mult,
+                op1=ALU.add,
+            )
+
+        def quantise_h(g):
+            h_codes[g] = work.tile([P, TOK], U32, align_bytes=64, tag="h_codes", name="h_codes%d" % g)
+            h_scales[g] = work.tile([P, TOK], U8, align_bytes=64, tag="h_scales", name="h_scales%d" % g)
+            nc.vector.quantize_mx(
+                out=h_codes[g][:].bitcast(FP8X4),
+                scales=h_scales[g][:],
+                in_=h_grouped[g][:].rearrange("p c t -> p (c t)"),
+            )
+
+        def regroup_w1(j):
+            w1_grouped[j] = const.tile([P, BANK, PACK], BF16, align_bytes=64, name="w1_grouped%d" % j)
+            if j % 2 == 0:
+                nc.gpsimd.tensor_scalar(
+                    out=w1_grouped[j][:],
+                    in0=w1_planes[j][:].rearrange("p t c -> p c t"),
+                    scalar1=1.0,
+                    scalar2=0.0,
+                    op0=ALU.mult,
+                    op1=ALU.add,
+                )
+            else:
+                dst, src = runs_of_four(w1_planes[j][:], w1_grouped[j][:])
+                nc.scalar.copy(out=dst, in_=src)
+
+        def quantise_w1(j):
+            cols = slice(j * BANK, (j + 1) * BANK)
+            nc.vector.quantize_mx(
+                out=w1_codes[:, cols].bitcast(FP8X4),
+                scales=w1_scales[:, cols],
+                in_=w1_grouped[j][:].rearrange("p c t -> p (c t)"),
+            )
+
+        def stage2(i):
+            g, s = divmod(i, GROUP)
+            toks = slice(s * P, (s + 1) * P)
+            act[i] = work.tile([P, HID], F32, tag="act", bufs=4, name="act%d" % i)
+            for j in range(N_BLOCKS):
+                cols = slice(j * BANK, (j + 1) * BANK)
+                o_ps = psum_o.tile([P, BANK], F32, tag="o")
+                nc.tensor.matmul_mx(
+                    out=o_ps[:],
+                    lhsT=h_codes[g][:, toks].bitcast(FP8X4),
+                    lhsT_scale=h_scales[g][:, toks],
+                    rhs=w1_codes[:, cols].bitcast(FP8X4),
+                    rhs_scale=w1_scales[:, cols],
+                    start=True,
+                    stop=True,
+                )
+                nc.vector.tensor_tensor(out=act[i][:, cols], in0=o_ps[:], in1=b1_bc[:, cols], op=ALU.add)
+
+        def gelu_and_store(i):
+            for half in range(HID // HALF):
+                cols = slice(half * HALF, (half + 1) * HALF)
+                nc.scalar.activation(out=act[i][:, cols], in_=act[i][:, cols], func=ACT.Gelu_apprx_tanh)
+                nc.sync.dma_start(out=out[i][:, cols], in_=act[i][:, cols])
+
+        dst, src = runs_of_four(wx_planes[:], wx_grouped[:])
+        nc.vector.tensor_copy(out=dst, in_=src)
+        transpose_h2(0)
+        posT_ps = psum_tp.tile([P, P], BF16, tag="tp")
+        nc.tensor.transpose(posT_ps[:], pos_sb[:], ident_b[:])
+        posT = const.tile([P, P], BF16)
+        nc.vector.tensor_copy(out=posT[:], in_=posT_ps[:])
+        nc.vector.quantize_mx(
+            out=wx_codes[:].bitcast(FP8X4),
+            scales=wx_scales[:],
+            in_=wx_grouped[:].rearrange("p c t -> p (c t)"),
+        )
+        quantise_h2(0)
+        gbT_ps = psum_tp.tile([P, P], BF16, tag="tp")
+        nc.tensor.transpose(gbT_ps[:], gb_rows[:], ident_b[:])
+        gb = const.tile([P, 2 * PACK], F32)
+        nc.vector.tensor_copy(out=gb[:], in_=gbT_ps[:, 0 : 2 * PACK])
+
+        PLANE_LAG = 3
+        W1_STEP = GROUP + 1
+        W1_LAG = 3
+        for k in range(B + PLANE_LAG + 1):
+            next_group = k // GROUP + 1
+            if next_group < N_GROUPS and k % GROUP == 2:
+                transpose_h2(next_group)
+            if k < B:
+                plain_part(k)
+            if next_group < N_GROUPS and k % GROUP == 3:
+                quantise_h2(next_group)
+            if 1 <= k <= B:
+                mx_part(k - 1)
+                centred_squares(k - 1)
+                if k % GROUP == 0:
+                    normalise(k // GROUP - 1)
+            if 0 <= k - W1_STEP < N_BLOCKS:
+                regroup_w1(k - W1_STEP)
+            if GROUP <= k - PLANE_LAG < B:
+                g, t = divmod(k - PLANE_LAG - GROUP, GROUP)
+                h_plane(g, t)
+                if t == PACK - 1:
+                    regroup_h(g)
+            if 0 <= k - W1_STEP - W1_LAG < N_BLOCKS:
+                quantise_w1(k - W1_STEP - W1_LAG)
+
+        for i in range(B + 1):
+            if i < B:
+                if i % GROUP == 0:
+                    quantise_h(i // GROUP)
+                stage2(i)
+            if i >= 1:
+                gelu_and_store(i - 1)
+            if 1 <= i <= PACK:
+                h_plane(N_GROUPS - 1, i - 1)
+                if i == PACK:
+                    regroup_h(N_GROUPS - 1)

@@ -68,10 +68,9 @@ def tile_gatblock_pb_kernel(
         pos_sb = const.tile([P, P], BF16)
         nc.sync.dma_start(out=pos_sb[:], in_=pos_mix)
         load_group(x_sb, x, 0)
-        xfb_bc = const.tile([P, D], BF16)
-        nc.sync.dma_start(out=xfb_bc[:], in_=xfeat_b.partition_broadcast(P))
         nc.sync.dma_start(out=gb_rows[0:PACK, :], in_=ln2_g.rearrange("(t p) -> t p", p=P))
         nc.sync.dma_start(out=gb_rows[PACK : 2 * PACK, :], in_=ln2_b.rearrange("(t p) -> t p", p=P))
+        nc.sync.dma_start(out=gb_rows[2 * PACK : 3 * PACK, :], in_=xfeat_b.rearrange("(t p) -> t p", p=P))
         load_group(h2_sb, h2, 1)
         load_group(h2_sb, h2, 2)
         load_group(x_sb, x, 1)
@@ -150,10 +149,19 @@ def tile_gatblock_pb_kernel(
         def plain_part(i):
             g, s = divmod(i, GROUP)
             t_ps = psum_t.tile([P, D], F32, tag="t")
-            nc.tensor.matmul(t_ps[:], lhsT=posT[:], rhs=h2_sb[g][:, s, :], start=True, stop=False)
+            for c in range(PACK):
+                nc.tensor.matmul(
+                    t_ps[:, c * P : (c + 1) * P],
+                    lhsT=gb[:, 2 * PACK + c : 2 * PACK + c + 1].to_broadcast([P, P]),
+                    rhs=ident_f[:],
+                    is_transpose=True,
+                    start=(c == 0),
+                    stop=False,
+                )
+            nc.tensor.matmul(t_ps[:], lhsT=posT[:], rhs=h2_sb[g][:, s, :], start=False, stop=False)
             nc.tensor.matmul(t_ps[:], lhsT=ident_b[:], rhs=x_sb[g][:, s, :], start=False, stop=True)
             t_sb[i] = work.tile([P, D], F32, tag="t_sb", bufs=3, name="t_sb%d" % i)
-            nc.vector.tensor_tensor(out=t_sb[i][:], in0=t_ps[:], in1=xfb_bc[:], op=ALU.add)
+            nc.scalar.copy(out=t_sb[i][:], in_=t_ps[:])
 
         def mx_part(i):
             g, s = divmod(i, GROUP)
@@ -261,7 +269,7 @@ def tile_gatblock_pb_kernel(
                 )
             else:
                 dst, src = runs_of_four(w1_planes[j][:], w1_grouped[j][:])
-                nc.scalar.copy(out=dst, in_=src)
+                nc.vector.tensor_copy(out=dst, in_=src)
 
         def quantise_w1(j):
             cols = slice(j * BANK, (j + 1) * BANK)
@@ -310,13 +318,16 @@ def tile_gatblock_pb_kernel(
         quantise_h2(0)
         gbT_ps = psum_tp.tile([P, P], BF16, tag="tp")
         nc.tensor.transpose(gbT_ps[:], gb_rows[:], ident_b[:])
-        gb = const.tile([P, 2 * PACK], F32)
-        nc.vector.tensor_copy(out=gb[:], in_=gbT_ps[:, 0 : 2 * PACK])
+        gb = const.tile([P, 3 * PACK], F32)
+        nc.vector.tensor_copy(out=gb[:], in_=gbT_ps[:, 0 : 3 * PACK])
 
-        PLANE_LAG = 3
-        W1_STEP = GROUP + 1
+        MX_LAG = 1
+        SQ_LAG = 2
+        W1_STEP = GROUP
         W1_LAG = 3
-        for k in range(B + PLANE_LAG + 1):
+        PLANE_LAG = 2 * GROUP
+        OUT_LAG = PLANE_LAG + GROUP + 1
+        for k in range(B + OUT_LAG + 1):
             next_group = k // GROUP + 1
             if next_group < N_GROUPS and k % GROUP == 2:
                 transpose_h2(next_group)
@@ -324,29 +335,24 @@ def tile_gatblock_pb_kernel(
                 plain_part(k)
             if next_group < N_GROUPS and k % GROUP == 3:
                 quantise_h2(next_group)
-            if 1 <= k <= B:
-                mx_part(k - 1)
-                centred_squares(k - 1)
-                if k % GROUP == 0:
-                    normalise(k // GROUP - 1)
+            if 0 <= k - MX_LAG < B:
+                mx_part(k - MX_LAG)
+            if 0 <= k - SQ_LAG < B:
+                centred_squares(k - SQ_LAG)
+                if (k - SQ_LAG) % GROUP == GROUP - 1:
+                    normalise((k - SQ_LAG) // GROUP)
             if 0 <= k - W1_STEP < N_BLOCKS:
                 regroup_w1(k - W1_STEP)
-            if GROUP <= k - PLANE_LAG < B:
-                g, t = divmod(k - PLANE_LAG - GROUP, GROUP)
+            if 0 <= k - PLANE_LAG < B:
+                g, t = divmod(k - PLANE_LAG, GROUP)
                 h_plane(g, t)
                 if t == PACK - 1:
                     regroup_h(g)
             if 0 <= k - W1_STEP - W1_LAG < N_BLOCKS:
                 quantise_w1(k - W1_STEP - W1_LAG)
-
-        for i in range(B + 1):
-            if i < B:
-                if i % GROUP == 0:
-                    quantise_h(i // GROUP)
-                stage2(i)
-            if i >= 1:
-                gelu_and_store(i - 1)
-            if 1 <= i <= PACK:
-                h_plane(N_GROUPS - 1, i - 1)
-                if i == PACK:
-                    regroup_h(N_GROUPS - 1)
+            if 0 <= k - OUT_LAG < B:
+                if (k - OUT_LAG) % GROUP == 0:
+                    quantise_h((k - OUT_LAG) // GROUP)
+                stage2(k - OUT_LAG)
+            if 0 <= k - OUT_LAG - 1 < B:
+                gelu_and_store(k - OUT_LAG - 1)

@@ -18,7 +18,8 @@ D = 512
 HID = 2048
 BANK = 512
 N_BLOCKS = HID // BANK
-GROUP = 4
+QUAD = 4
+GROUP = 2
 N_GROUPS = B // GROUP
 TOK = GROUP * P
 HALF = HID // 2
@@ -47,18 +48,18 @@ def tile_gatblock_pb_kernel(
         psum_o = stack.enter_context(tc.psum_pool(name="psum_o", bufs=3))
         stack.enter_context(tc.manual_schedule())
 
-        h2_sb = [const.tile([P, GROUP, D], BF16, name="h2_sb%d" % g) for g in range(N_GROUPS)]
-        x_sb = [const.tile([P, GROUP, D], BF16, name="x_sb%d" % g) for g in range(N_GROUPS)]
+        h2_sb = [const.tile([P, QUAD, D], BF16, name="h2_sb%d" % q) for q in range(B // QUAD)]
+        x_sb = [const.tile([P, QUAD, D], BF16, name="x_sb%d" % q) for q in range(B // QUAD)]
 
-        def load_group(dst, src, g):
+        def load_quad(dst, src, q):
             nc.sync.dma_start(
-                out=dst[g][:], in_=src[g * GROUP : (g + 1) * GROUP].rearrange("b n d -> n b d")
+                out=dst[q][:], in_=src[q * QUAD : (q + 1) * QUAD].rearrange("b n d -> n b d")
             )
 
         gb_rows = const.tile([P, P], BF16)
         nc.vector.memset(gb_rows[:], 0.0)
 
-        load_group(h2_sb, h2, 0)
+        load_quad(h2_sb, h2, 0)
         wx_planes = const.tile([P, PACK, D], BF16)
         for u in range(2):
             nc.sync.dma_start(
@@ -67,13 +68,12 @@ def tile_gatblock_pb_kernel(
             )
         pos_sb = const.tile([P, P], BF16)
         nc.sync.dma_start(out=pos_sb[:], in_=pos_mix)
-        load_group(x_sb, x, 0)
         nc.sync.dma_start(out=gb_rows[0:PACK, :], in_=ln2_g.rearrange("(t p) -> t p", p=P))
         nc.sync.dma_start(out=gb_rows[PACK : 2 * PACK, :], in_=ln2_b.rearrange("(t p) -> t p", p=P))
         nc.sync.dma_start(out=gb_rows[2 * PACK : 3 * PACK, :], in_=xfeat_b.rearrange("(t p) -> t p", p=P))
-        load_group(h2_sb, h2, 1)
-        load_group(h2_sb, h2, 2)
-        load_group(x_sb, x, 1)
+        load_quad(x_sb, x, 0)
+        load_quad(h2_sb, h2, 1)
+        load_quad(x_sb, x, 1)
         w1_planes = []
         for j in range(N_BLOCKS):
             w1p = const.tile([P, PACK, BANK], BF16, name="w1_planes%d" % j)
@@ -82,9 +82,10 @@ def tile_gatblock_pb_kernel(
                 in_=mlp_w1[:, j * BANK : (j + 1) * BANK].rearrange("(t p) n -> p t n", p=P),
             )
             w1_planes.append(w1p)
-        load_group(x_sb, x, 2)
         b1_bc = const.tile([P, HID], BF16)
         nc.sync.dma_start(out=b1_bc[:], in_=mlp_b1.partition_broadcast(P))
+        load_quad(h2_sb, h2, 2)
+        load_quad(x_sb, x, 2)
 
         warm = const.tile([P, 1], F32)
         nc.vector.memset(warm[:], 0.0)
@@ -121,33 +122,29 @@ def tile_gatblock_pb_kernel(
         act = [None] * B
 
         def transpose_h2(g):
-            h2_words = h2_sb[g][:].rearrange("p b d -> p (b d)").bitcast(F32)
-            h2_grouped[g] = work.tile([P, TOK * PACK], BF16, align_bytes=64, tag="h2g", name="h2g%d" % g)
-            grouped_words = h2_grouped[g][:].bitcast(F32).rearrange("p (n u) -> p n u", u=2)
-            for half in range(2):
-                h2T_ps = psum_tp.tile([P, 2, 2 * P], F32, tag="tp")
-                for s2 in range(2):
-                    for u in range(2):
-                        first = (2 * half + s2) * (D // 2) + u * P
-                        nc.tensor.transpose(
-                            h2T_ps[:, u, s2 * P : (s2 + 1) * P],
-                            h2_words[:, first : first + P],
-                            ident_f[:],
-                        )
-                nc.scalar.copy(
-                    out=grouped_words[:, half * 2 * P : (half + 1) * 2 * P, :],
-                    in_=h2T_ps[:].rearrange("p u n -> p n u"),
-                )
+            h2_grouped[g] = work.tile([P, TOK * PACK], BF16, align_bytes=64, tag="h2g", bufs=3, name="h2g%d" % g)
+            h2T_ps = psum_tp.tile([P, 2, TOK], F32, tag="tp")
+            for s in range(GROUP):
+                q, r = divmod(g * GROUP + s, QUAD)
+                h2_words = h2_sb[q][:, r, :].bitcast(F32)
+                for u in range(2):
+                    nc.tensor.transpose(
+                        h2T_ps[:, u, s * P : (s + 1) * P], h2_words[:, u * P : (u + 1) * P], ident_f[:]
+                    )
+            nc.scalar.copy(
+                out=h2_grouped[g][:].bitcast(F32).rearrange("p (n u) -> p n u", u=2),
+                in_=h2T_ps[:].rearrange("p u n -> p n u"),
+            )
 
         def quantise_h2(g):
-            h2_codes[g] = work.tile([P, TOK], U32, align_bytes=64, tag="h2c", name="h2c%d" % g)
-            h2_scales[g] = work.tile([P, TOK], U8, align_bytes=64, tag="h2s", name="h2s%d" % g)
+            h2_codes[g] = work.tile([P, TOK], U32, align_bytes=64, tag="h2c", bufs=3, name="h2c%d" % g)
+            h2_scales[g] = work.tile([P, TOK], U8, align_bytes=64, tag="h2s", bufs=3, name="h2s%d" % g)
             nc.vector.quantize_mx(
                 out=h2_codes[g][:].bitcast(FP8X4), scales=h2_scales[g][:], in_=h2_grouped[g][:]
             )
 
         def plain_part(i):
-            g, s = divmod(i, GROUP)
+            q, r = divmod(i, QUAD)
             t_ps = psum_t.tile([P, D], F32, tag="t")
             for c in range(PACK):
                 nc.tensor.matmul(
@@ -158,8 +155,8 @@ def tile_gatblock_pb_kernel(
                     start=(c == 0),
                     stop=False,
                 )
-            nc.tensor.matmul(t_ps[:], lhsT=posT[:], rhs=h2_sb[g][:, s, :], start=False, stop=False)
-            nc.tensor.matmul(t_ps[:], lhsT=ident_b[:], rhs=x_sb[g][:, s, :], start=False, stop=True)
+            nc.tensor.matmul(t_ps[:], lhsT=posT[:], rhs=h2_sb[q][:, r, :], start=False, stop=False)
+            nc.tensor.matmul(t_ps[:], lhsT=ident_b[:], rhs=x_sb[q][:, r, :], start=False, stop=True)
             t_sb[i] = work.tile([P, D], F32, tag="t_sb", bufs=3, name="t_sb%d" % i)
             nc.scalar.copy(out=t_sb[i][:], in_=t_ps[:])
 
@@ -176,7 +173,7 @@ def tile_gatblock_pb_kernel(
                 start=True,
                 stop=True,
             )
-            x1[i] = work.tile([P, D], F32, tag="x1", bufs=2 * GROUP, name="x1_%d" % i)
+            x1[i] = work.tile([P, D], F32, tag="x1", bufs=6, name="x1_%d" % i)
             nc.vector.scalar_tensor_tensor(
                 out=x1[i][:],
                 in0=y_ps[:],
@@ -190,7 +187,7 @@ def tile_gatblock_pb_kernel(
         def centred_squares(i):
             g, s = divmod(i, GROUP)
             col = slice(s, s + 1)
-            squares = work.tile([P, D], BF16, tag="squares", bufs=GROUP)
+            squares = work.tile([P, D], BF16, tag="squares", bufs=4)
             nc.scalar.activation(
                 out=squares[:],
                 in_=x1[i][:],
@@ -210,7 +207,7 @@ def tile_gatblock_pb_kernel(
             nc.gpsimd.tensor_tensor(out=rstd[g][:], in0=var_eps[g][:], in1=neg_half[:], op=ALU.pow)
             for s in range(GROUP):
                 i = g * GROUP + s
-                normed[i] = work.tile([P, D], F32, tag="normed", bufs=2 * GROUP, name="normed%d" % i)
+                normed[i] = work.tile([P, D], F32, tag="normed", bufs=8, name="normed%d" % i)
                 nc.gpsimd.tensor_scalar(
                     out=normed[i][:],
                     in0=x1[i][:],
@@ -222,7 +219,7 @@ def tile_gatblock_pb_kernel(
 
         def h_plane(g, t):
             if t == 0:
-                h_planes[g] = work.tile([P, PACK, TOK], BF16, tag="h_planes", name="h_planes%d" % g)
+                h_planes[g] = work.tile([P, PACK, TOK], BF16, tag="h_planes", bufs=3, name="h_planes%d" % g)
             nT_ps = psum_tp.tile([P, TOK], F32, tag="tp")
             for s in range(GROUP):
                 nc.tensor.transpose(
@@ -237,7 +234,7 @@ def tile_gatblock_pb_kernel(
             )
 
         def regroup_h(g):
-            h_grouped[g] = work.tile([P, TOK, PACK], BF16, align_bytes=64, tag="h_grouped", name="h_grouped%d" % g)
+            h_grouped[g] = work.tile([P, TOK, PACK], BF16, align_bytes=64, tag="h_grouped", bufs=3, name="h_grouped%d" % g)
             nc.gpsimd.tensor_scalar(
                 out=h_grouped[g][:],
                 in0=h_planes[g][:].rearrange("p t c -> p c t"),
@@ -248,8 +245,8 @@ def tile_gatblock_pb_kernel(
             )
 
         def quantise_h(g):
-            h_codes[g] = work.tile([P, TOK], U32, align_bytes=64, tag="h_codes", name="h_codes%d" % g)
-            h_scales[g] = work.tile([P, TOK], U8, align_bytes=64, tag="h_scales", name="h_scales%d" % g)
+            h_codes[g] = work.tile([P, TOK], U32, align_bytes=64, tag="h_codes", bufs=3, name="h_codes%d" % g)
+            h_scales[g] = work.tile([P, TOK], U8, align_bytes=64, tag="h_scales", bufs=3, name="h_scales%d" % g)
             nc.vector.quantize_mx(
                 out=h_codes[g][:].bitcast(FP8X4),
                 scales=h_scales[g][:],
@@ -258,18 +255,8 @@ def tile_gatblock_pb_kernel(
 
         def regroup_w1(j):
             w1_grouped[j] = const.tile([P, BANK, PACK], BF16, align_bytes=64, name="w1_grouped%d" % j)
-            if j % 2 == 0:
-                nc.gpsimd.tensor_scalar(
-                    out=w1_grouped[j][:],
-                    in0=w1_planes[j][:].rearrange("p t c -> p c t"),
-                    scalar1=1.0,
-                    scalar2=0.0,
-                    op0=ALU.mult,
-                    op1=ALU.add,
-                )
-            else:
-                dst, src = runs_of_four(w1_planes[j][:], w1_grouped[j][:])
-                nc.vector.tensor_copy(out=dst, in_=src)
+            dst, src = runs_of_four(w1_planes[j][:], w1_grouped[j][:])
+            nc.vector.tensor_copy(out=dst, in_=src)
 
         def quantise_w1(j):
             cols = slice(j * BANK, (j + 1) * BANK)
@@ -323,17 +310,18 @@ def tile_gatblock_pb_kernel(
 
         MX_LAG = 1
         SQ_LAG = 2
-        W1_STEP = GROUP
+        W1_STEP = 3
         W1_LAG = 3
-        PLANE_LAG = 2 * GROUP
-        OUT_LAG = PLANE_LAG + GROUP + 1
+        PLANE_LAG = 6
+        OUT_LAG = 10
+        PLANES_A_STEP = PACK // GROUP
         for k in range(B + OUT_LAG + 1):
             next_group = k // GROUP + 1
-            if next_group < N_GROUPS and k % GROUP == 2:
+            if next_group < N_GROUPS and k % GROUP == 0:
                 transpose_h2(next_group)
             if k < B:
                 plain_part(k)
-            if next_group < N_GROUPS and k % GROUP == 3:
+            if next_group < N_GROUPS and k % GROUP == GROUP - 1:
                 quantise_h2(next_group)
             if 0 <= k - MX_LAG < B:
                 mx_part(k - MX_LAG)
@@ -344,15 +332,16 @@ def tile_gatblock_pb_kernel(
             if 0 <= k - W1_STEP < N_BLOCKS:
                 regroup_w1(k - W1_STEP)
             if 0 <= k - PLANE_LAG < B:
-                g, t = divmod(k - PLANE_LAG, GROUP)
-                h_plane(g, t)
-                if t == PACK - 1:
+                g, s = divmod(k - PLANE_LAG, GROUP)
+                for t in range(s * PLANES_A_STEP, (s + 1) * PLANES_A_STEP):
+                    h_plane(g, t)
+                if s == GROUP - 1:
                     regroup_h(g)
             if 0 <= k - W1_STEP - W1_LAG < N_BLOCKS:
                 quantise_w1(k - W1_STEP - W1_LAG)
+            if 0 <= k - OUT_LAG + 1 < B and (k - OUT_LAG + 1) % GROUP == 0:
+                quantise_h((k - OUT_LAG + 1) // GROUP)
             if 0 <= k - OUT_LAG < B:
-                if (k - OUT_LAG) % GROUP == 0:
-                    quantise_h((k - OUT_LAG) // GROUP)
                 stage2(k - OUT_LAG)
             if 0 <= k - OUT_LAG - 1 < B:
                 gelu_and_store(k - OUT_LAG - 1)

@@ -42,10 +42,7 @@ def tile_gatblock_pb_kernel(
     with ExitStack() as stack:
         const = stack.enter_context(tc.tile_pool(name="const", bufs=1))
         work = stack.enter_context(tc.tile_pool(name="work", bufs=2))
-        psum_tp = stack.enter_context(tc.psum_pool(name="psum_tp", bufs=2))
-        psum_t = stack.enter_context(tc.psum_pool(name="psum_t", bufs=2))
-        psum_y = stack.enter_context(tc.psum_pool(name="psum_y", bufs=1))
-        psum_o = stack.enter_context(tc.psum_pool(name="psum_o", bufs=3))
+        psum = stack.enter_context(tc.psum_pool(name="psum", bufs=8))
         stack.enter_context(tc.manual_schedule())
 
         h2_sb = [const.tile([P, QUAD, D], BF16, name="h2_sb%d" % q) for q in range(B // QUAD)]
@@ -82,10 +79,10 @@ def tile_gatblock_pb_kernel(
                 in_=mlp_w1[:, j * BANK : (j + 1) * BANK].rearrange("(t p) n -> p t n", p=P),
             )
             w1_planes.append(w1p)
-        b1_bc = const.tile([P, HID], BF16)
-        nc.sync.dma_start(out=b1_bc[:], in_=mlp_b1.partition_broadcast(P))
         load_quad(h2_sb, h2, 2)
         load_quad(x_sb, x, 2)
+        b1_bc = const.tile([P, HID], BF16)
+        nc.sync.dma_start(out=b1_bc[:], in_=mlp_b1.partition_broadcast(P))
 
         warm = const.tile([P, 1], F32)
         nc.vector.memset(warm[:], 0.0)
@@ -123,7 +120,7 @@ def tile_gatblock_pb_kernel(
 
         def transpose_h2(g):
             h2_grouped[g] = work.tile([P, TOK * PACK], BF16, align_bytes=64, tag="h2g", bufs=3, name="h2g%d" % g)
-            h2T_ps = psum_tp.tile([P, 2, TOK], F32, tag="tp")
+            h2T_ps = psum.tile([P, 2, TOK], F32, tag="bank")
             for s in range(GROUP):
                 q, r = divmod(g * GROUP + s, QUAD)
                 h2_words = h2_sb[q][:, r, :].bitcast(F32)
@@ -145,7 +142,7 @@ def tile_gatblock_pb_kernel(
 
         def plain_part(i):
             q, r = divmod(i, QUAD)
-            t_ps = psum_t.tile([P, D], F32, tag="t")
+            t_ps = psum.tile([P, D], F32, tag="bank")
             for c in range(PACK):
                 nc.tensor.matmul(
                     t_ps[:, c * P : (c + 1) * P],
@@ -163,7 +160,7 @@ def tile_gatblock_pb_kernel(
         def mx_part(i):
             g, s = divmod(i, GROUP)
             toks = slice(s * P, (s + 1) * P)
-            y_ps = psum_y.tile([P, D], F32, tag="y")
+            y_ps = psum.tile([P, D], F32, tag="bank")
             nc.tensor.matmul_mx(
                 out=y_ps[:],
                 lhsT=h2_codes[g][:, toks].bitcast(FP8X4),
@@ -220,7 +217,7 @@ def tile_gatblock_pb_kernel(
         def h_plane(g, t):
             if t == 0:
                 h_planes[g] = work.tile([P, PACK, TOK], BF16, tag="h_planes", bufs=3, name="h_planes%d" % g)
-            nT_ps = psum_tp.tile([P, TOK], F32, tag="tp")
+            nT_ps = psum.tile([P, TOK], F32, tag="bank")
             for s in range(GROUP):
                 nc.tensor.transpose(
                     nT_ps[:, s * P : (s + 1) * P], normed[g * GROUP + s][:, t * P : (t + 1) * P], ident_f[:]
@@ -272,7 +269,7 @@ def tile_gatblock_pb_kernel(
             act[i] = work.tile([P, HID], F32, tag="act", bufs=4, name="act%d" % i)
             for j in range(N_BLOCKS):
                 cols = slice(j * BANK, (j + 1) * BANK)
-                o_ps = psum_o.tile([P, BANK], F32, tag="o")
+                o_ps = psum.tile([P, BANK], F32, tag="bank")
                 nc.tensor.matmul_mx(
                     out=o_ps[:],
                     lhsT=h_codes[g][:, toks].bitcast(FP8X4),
@@ -293,7 +290,7 @@ def tile_gatblock_pb_kernel(
         dst, src = runs_of_four(wx_planes[:], wx_grouped[:])
         nc.vector.tensor_copy(out=dst, in_=src)
         transpose_h2(0)
-        posT_ps = psum_tp.tile([P, P], BF16, tag="tp")
+        posT_ps = psum.tile([P, P], BF16, tag="bank")
         nc.tensor.transpose(posT_ps[:], pos_sb[:], ident_b[:])
         posT = const.tile([P, P], BF16)
         nc.vector.tensor_copy(out=posT[:], in_=posT_ps[:])
@@ -303,7 +300,7 @@ def tile_gatblock_pb_kernel(
             in_=wx_grouped[:].rearrange("p c t -> p (c t)"),
         )
         quantise_h2(0)
-        gbT_ps = psum_tp.tile([P, P], BF16, tag="tp")
+        gbT_ps = psum.tile([P, P], BF16, tag="bank")
         nc.tensor.transpose(gbT_ps[:], gb_rows[:], ident_b[:])
         gb = const.tile([P, 3 * PACK], F32)
         nc.vector.tensor_copy(out=gb[:], in_=gbT_ps[:, 0 : 3 * PACK])
@@ -313,7 +310,7 @@ def tile_gatblock_pb_kernel(
         W1_STEP = 3
         W1_LAG = 3
         PLANE_LAG = 6
-        OUT_LAG = 10
+        OUT_LAG = 11
         PLANES_A_STEP = PACK // GROUP
         for k in range(B + OUT_LAG + 1):
             next_group = k // GROUP + 1

@@ -18,10 +18,11 @@ D = 512
 HID = 2048
 BANK = 512
 N_BLOCKS = HID // BANK
-QUAD = 4
 GROUP = 2
 N_GROUPS = B // GROUP
 TOK = GROUP * P
+PLANES_A_BANK = BANK // TOK
+EARLY_GROUPS = 4
 HALF = HID // 2
 EPS = 1e-5
 
@@ -45,32 +46,33 @@ def tile_gatblock_pb_kernel(
         psum = stack.enter_context(tc.psum_pool(name="psum", bufs=8))
         stack.enter_context(tc.manual_schedule())
 
-        h2_sb = [const.tile([P, QUAD, D], BF16, name="h2_sb%d" % q) for q in range(B // QUAD)]
-        x_sb = [const.tile([P, QUAD, D], BF16, name="x_sb%d" % q) for q in range(B // QUAD)]
+        h2_sb = [const.tile([P, GROUP, D], BF16, name="h2_sb%d" % g) for g in range(N_GROUPS)]
+        x_sb = [const.tile([P, GROUP, D], BF16, name="x_sb%d" % g) for g in range(N_GROUPS)]
 
-        def load_quad(dst, src, q):
+        def load_group(dst, src, g):
             nc.sync.dma_start(
-                out=dst[q][:], in_=src[q * QUAD : (q + 1) * QUAD].rearrange("b n d -> n b d")
+                out=dst[g][:], in_=src[g * GROUP : (g + 1) * GROUP].rearrange("b n d -> n b d")
             )
 
         gb_rows = const.tile([P, P], BF16)
         nc.vector.memset(gb_rows[:], 0.0)
 
-        load_quad(h2_sb, h2, 0)
         wx_planes = const.tile([P, PACK, D], BF16)
         for u in range(2):
             nc.sync.dma_start(
                 out=wx_planes[:, 2 * u : 2 * u + 2, :],
                 in_=xfeat_w[256 * u : 256 * (u + 1), :].rearrange("(q e) c -> q e c", e=2),
             )
+        load_group(h2_sb, h2, 0)
         pos_sb = const.tile([P, P], BF16)
         nc.sync.dma_start(out=pos_sb[:], in_=pos_mix)
         nc.sync.dma_start(out=gb_rows[0:PACK, :], in_=ln2_g.rearrange("(t p) -> t p", p=P))
         nc.sync.dma_start(out=gb_rows[PACK : 2 * PACK, :], in_=ln2_b.rearrange("(t p) -> t p", p=P))
         nc.sync.dma_start(out=gb_rows[2 * PACK : 3 * PACK, :], in_=xfeat_b.rearrange("(t p) -> t p", p=P))
-        load_quad(x_sb, x, 0)
-        load_quad(h2_sb, h2, 1)
-        load_quad(x_sb, x, 1)
+        load_group(x_sb, x, 0)
+        for g in range(1, EARLY_GROUPS):
+            load_group(h2_sb, h2, g)
+            load_group(x_sb, x, g)
         w1_planes = []
         for j in range(N_BLOCKS):
             w1p = const.tile([P, PACK, BANK], BF16, name="w1_planes%d" % j)
@@ -79,8 +81,9 @@ def tile_gatblock_pb_kernel(
                 in_=mlp_w1[:, j * BANK : (j + 1) * BANK].rearrange("(t p) n -> p t n", p=P),
             )
             w1_planes.append(w1p)
-        load_quad(h2_sb, h2, 2)
-        load_quad(x_sb, x, 2)
+        for g in range(EARLY_GROUPS, N_GROUPS):
+            load_group(h2_sb, h2, g)
+            load_group(x_sb, x, g)
         b1_bc = const.tile([P, HID], BF16)
         nc.sync.dma_start(out=b1_bc[:], in_=mlp_b1.partition_broadcast(P))
 
@@ -113,6 +116,7 @@ def tile_gatblock_pb_kernel(
         h_grouped = [None] * N_GROUPS
         h_codes = [None] * N_GROUPS
         h_scales = [None] * N_GROUPS
+        t_ps = [None] * B
         t_sb = [None] * B
         x1 = [None] * B
         normed = [None] * B
@@ -122,8 +126,7 @@ def tile_gatblock_pb_kernel(
             h2_grouped[g] = work.tile([P, TOK * PACK], BF16, align_bytes=64, tag="h2g", bufs=3, name="h2g%d" % g)
             h2T_ps = psum.tile([P, 2, TOK], F32, tag="bank")
             for s in range(GROUP):
-                q, r = divmod(g * GROUP + s, QUAD)
-                h2_words = h2_sb[q][:, r, :].bitcast(F32)
+                h2_words = h2_sb[g][:, s, :].bitcast(F32)
                 for u in range(2):
                     nc.tensor.transpose(
                         h2T_ps[:, u, s * P : (s + 1) * P], h2_words[:, u * P : (u + 1) * P], ident_f[:]
@@ -140,22 +143,24 @@ def tile_gatblock_pb_kernel(
                 out=h2_codes[g][:].bitcast(FP8X4), scales=h2_scales[g][:], in_=h2_grouped[g][:]
             )
 
-        def plain_part(i):
-            q, r = divmod(i, QUAD)
-            t_ps = psum.tile([P, D], F32, tag="bank")
+        def bias_part(i):
+            t_ps[i] = psum.tile([P, D], F32, tag="bank", name="t_ps%d" % i)
             for c in range(PACK):
                 nc.tensor.matmul(
-                    t_ps[:, c * P : (c + 1) * P],
+                    t_ps[i][:, c * P : (c + 1) * P],
                     lhsT=gb[:, 2 * PACK + c : 2 * PACK + c + 1].to_broadcast([P, P]),
                     rhs=ident_f[:],
                     is_transpose=True,
                     start=(c == 0),
                     stop=False,
                 )
-            nc.tensor.matmul(t_ps[:], lhsT=posT[:], rhs=h2_sb[q][:, r, :], start=False, stop=False)
-            nc.tensor.matmul(t_ps[:], lhsT=ident_b[:], rhs=x_sb[q][:, r, :], start=False, stop=True)
+
+        def plain_part(i):
+            g, s = divmod(i, GROUP)
+            nc.tensor.matmul(t_ps[i][:], lhsT=posT[:], rhs=h2_sb[g][:, s, :], start=False, stop=False)
+            nc.tensor.matmul(t_ps[i][:], lhsT=ident_b[:], rhs=x_sb[g][:, s, :], start=False, stop=True)
             t_sb[i] = work.tile([P, D], F32, tag="t_sb", bufs=3, name="t_sb%d" % i)
-            nc.scalar.copy(out=t_sb[i][:], in_=t_ps[:])
+            nc.scalar.copy(out=t_sb[i][:], in_=t_ps[i][:])
 
         def mx_part(i):
             g, s = divmod(i, GROUP)
@@ -214,21 +219,25 @@ def tile_gatblock_pb_kernel(
                     op1=ALU.mult,
                 )
 
-        def h_plane(g, t):
-            if t == 0:
+        def h_planes_bank(g, first):
+            if first == 0:
                 h_planes[g] = work.tile([P, PACK, TOK], BF16, tag="h_planes", bufs=3, name="h_planes%d" % g)
-            nT_ps = psum.tile([P, TOK], F32, tag="bank")
-            for s in range(GROUP):
-                nc.tensor.transpose(
-                    nT_ps[:, s * P : (s + 1) * P], normed[g * GROUP + s][:, t * P : (t + 1) * P], ident_f[:]
+            nT_ps = psum.tile([P, PLANES_A_BANK, TOK], F32, tag="bank")
+            for j in range(PLANES_A_BANK):
+                t = first + j
+                for s in range(GROUP):
+                    nc.tensor.transpose(
+                        nT_ps[:, j, s * P : (s + 1) * P], normed[g * GROUP + s][:, t * P : (t + 1) * P], ident_f[:]
+                    )
+            for j in range(PLANES_A_BANK):
+                t = first + j
+                nc.scalar.activation(
+                    out=h_planes[g][:, t, :],
+                    in_=nT_ps[:, j, :],
+                    func=ACT.Identity,
+                    scale=gb[:, t : t + 1],
+                    bias=gb[:, PACK + t : PACK + t + 1],
                 )
-            nc.scalar.activation(
-                out=h_planes[g][:, t, :],
-                in_=nT_ps[:],
-                func=ACT.Identity,
-                scale=gb[:, t : t + 1],
-                bias=gb[:, PACK + t : PACK + t + 1],
-            )
 
         def regroup_h(g):
             h_grouped[g] = work.tile([P, TOK, PACK], BF16, align_bytes=64, tag="h_grouped", bufs=3, name="h_grouped%d" % g)
@@ -294,16 +303,16 @@ def tile_gatblock_pb_kernel(
         nc.tensor.transpose(posT_ps[:], pos_sb[:], ident_b[:])
         posT = const.tile([P, P], BF16)
         nc.vector.tensor_copy(out=posT[:], in_=posT_ps[:])
+        gbT_ps = psum.tile([P, P], BF16, tag="bank")
+        nc.tensor.transpose(gbT_ps[:], gb_rows[:], ident_b[:])
+        gb = const.tile([P, 3 * PACK], F32)
+        nc.vector.tensor_copy(out=gb[:], in_=gbT_ps[:, 0 : 3 * PACK])
         nc.vector.quantize_mx(
             out=wx_codes[:].bitcast(FP8X4),
             scales=wx_scales[:],
             in_=wx_grouped[:].rearrange("p c t -> p (c t)"),
         )
         quantise_h2(0)
-        gbT_ps = psum.tile([P, P], BF16, tag="bank")
-        nc.tensor.transpose(gbT_ps[:], gb_rows[:], ident_b[:])
-        gb = const.tile([P, 3 * PACK], F32)
-        nc.vector.tensor_copy(out=gb[:], in_=gbT_ps[:, 0 : 3 * PACK])
 
         MX_LAG = 1
         SQ_LAG = 2
@@ -311,13 +320,13 @@ def tile_gatblock_pb_kernel(
         W1_LAG = 3
         PLANE_LAG = 6
         OUT_LAG = 11
-        PLANES_A_STEP = PACK // GROUP
         for k in range(B + OUT_LAG + 1):
             next_group = k // GROUP + 1
+            if k < B:
+                bias_part(k)
+                plain_part(k)
             if next_group < N_GROUPS and k % GROUP == 0:
                 transpose_h2(next_group)
-            if k < B:
-                plain_part(k)
             if next_group < N_GROUPS and k % GROUP == GROUP - 1:
                 quantise_h2(next_group)
             if 0 <= k - MX_LAG < B:
@@ -330,8 +339,7 @@ def tile_gatblock_pb_kernel(
                 regroup_w1(k - W1_STEP)
             if 0 <= k - PLANE_LAG < B:
                 g, s = divmod(k - PLANE_LAG, GROUP)
-                for t in range(s * PLANES_A_STEP, (s + 1) * PLANES_A_STEP):
-                    h_plane(g, t)
+                h_planes_bank(g, s * PLANES_A_BANK)
                 if s == GROUP - 1:
                     regroup_h(g)
             if 0 <= k - W1_STEP - W1_LAG < N_BLOCKS:

@@ -64,12 +64,12 @@ def tile_gatblock_pb_kernel(
                 in_=xfeat_w[256 * u : 256 * (u + 1), :].rearrange("(q e) c -> q e c", e=2),
             )
         load_group(h2_sb, h2, 0)
-        pos_sb = const.tile([P, P], BF16)
-        nc.sync.dma_start(out=pos_sb[:], in_=pos_mix)
-        nc.sync.dma_start(out=gb_rows[0:PACK, :], in_=ln2_g.rearrange("(t p) -> t p", p=P))
-        nc.sync.dma_start(out=gb_rows[PACK : 2 * PACK, :], in_=ln2_b.rearrange("(t p) -> t p", p=P))
-        nc.sync.dma_start(out=gb_rows[2 * PACK : 3 * PACK, :], in_=xfeat_b.rearrange("(t p) -> t p", p=P))
         load_group(x_sb, x, 0)
+        pos_sb = const.tile([P, P], BF16)
+        nc.scalar.dma_start(out=pos_sb[:], in_=pos_mix)
+        nc.scalar.dma_start(out=gb_rows[0:PACK, :], in_=ln2_g.rearrange("(t p) -> t p", p=P))
+        nc.scalar.dma_start(out=gb_rows[PACK : 2 * PACK, :], in_=ln2_b.rearrange("(t p) -> t p", p=P))
+        nc.scalar.dma_start(out=gb_rows[2 * PACK : 3 * PACK, :], in_=xfeat_b.rearrange("(t p) -> t p", p=P))
         for g in range(1, EARLY_GROUPS):
             load_group(h2_sb, h2, g)
             load_group(x_sb, x, g)

@@ -22,11 +22,27 @@ GROUP = 2
 N_GROUPS = B // GROUP
 TOK = GROUP * P
 PLANES_A_BANK = BANK // TOK
-EARLY_GROUPS = 4
+EARLY_GROUPS = 3
 HALF = HID // 2
 EPS = 1e-5
 
 FLOPS = 2 * B * P * (D * D + D * HID + P * D)
+
+
+TAG_H2 = TAG_T = TAG_Y = TAG_N = TAG_O = "bank"
+PSUM_BUFS = 8
+
+
+def H2_ON_V(g):
+    return False
+
+
+def PLANES_ON_V(g, first):
+    return g > 1 and first > 0
+
+
+def W1_ON_G(j):
+    return False
 
 
 def runs_of_four(planes, grouped):
@@ -43,7 +59,7 @@ def tile_gatblock_pb_kernel(
     with ExitStack() as stack:
         const = stack.enter_context(tc.tile_pool(name="const", bufs=1))
         work = stack.enter_context(tc.tile_pool(name="work", bufs=2))
-        psum = stack.enter_context(tc.psum_pool(name="psum", bufs=8))
+        psum = stack.enter_context(tc.psum_pool(name="psum", bufs=PSUM_BUFS))
         stack.enter_context(tc.manual_schedule())
 
         h2_sb = [const.tile([P, GROUP, D], BF16, name="h2_sb%d" % g) for g in range(N_GROUPS)]
@@ -117,23 +133,29 @@ def tile_gatblock_pb_kernel(
         h_codes = [None] * N_GROUPS
         h_scales = [None] * N_GROUPS
         t_ps = [None] * B
+        y = [None] * B
+        h2T = [None] * N_GROUPS
+        nT = {}
         t_sb = [None] * B
         x1 = [None] * B
         normed = [None] * B
         act = [None] * B
 
         def transpose_h2(g):
-            h2_grouped[g] = work.tile([P, TOK * PACK], BF16, align_bytes=64, tag="h2g", bufs=3, name="h2g%d" % g)
-            h2T_ps = psum.tile([P, 2, TOK], F32, tag="bank")
+            h2T_ps = psum.tile([P, 2, TOK], F32, tag=TAG_H2)
+            h2T[g] = h2T_ps
             for s in range(GROUP):
                 h2_words = h2_sb[g][:, s, :].bitcast(F32)
                 for u in range(2):
                     nc.tensor.transpose(
                         h2T_ps[:, u, s * P : (s + 1) * P], h2_words[:, u * P : (u + 1) * P], ident_f[:]
                     )
-            nc.scalar.copy(
+
+        def empty_h2(g):
+            h2_grouped[g] = work.tile([P, TOK * PACK], BF16, align_bytes=64, tag="h2g", bufs=3, name="h2g%d" % g)
+            (nc.vector.tensor_copy if H2_ON_V(g) else nc.scalar.copy)(
                 out=h2_grouped[g][:].bitcast(F32).rearrange("p (n u) -> p n u", u=2),
-                in_=h2T_ps[:].rearrange("p u n -> p n u"),
+                in_=h2T[g][:].rearrange("p u n -> p n u"),
             )
 
         def quantise_h2(g):
@@ -144,7 +166,7 @@ def tile_gatblock_pb_kernel(
             )
 
         def bias_part(i):
-            t_ps[i] = psum.tile([P, D], F32, tag="bank", name="t_ps%d" % i)
+            t_ps[i] = psum.tile([P, D], F32, tag=TAG_T, name="t_ps%d" % i)
             for c in range(PACK):
                 nc.tensor.matmul(
                     t_ps[i][:, c * P : (c + 1) * P],
@@ -159,13 +181,16 @@ def tile_gatblock_pb_kernel(
             g, s = divmod(i, GROUP)
             nc.tensor.matmul(t_ps[i][:], lhsT=posT[:], rhs=h2_sb[g][:, s, :], start=False, stop=False)
             nc.tensor.matmul(t_ps[i][:], lhsT=ident_b[:], rhs=x_sb[g][:, s, :], start=False, stop=True)
+
+        def empty_t(i):
             t_sb[i] = work.tile([P, D], F32, tag="t_sb", bufs=3, name="t_sb%d" % i)
             nc.scalar.copy(out=t_sb[i][:], in_=t_ps[i][:])
 
         def mx_part(i):
             g, s = divmod(i, GROUP)
             toks = slice(s * P, (s + 1) * P)
-            y_ps = psum.tile([P, D], F32, tag="bank")
+            y_ps = psum.tile([P, D], F32, tag=TAG_Y)
+            y[i] = y_ps
             nc.tensor.matmul_mx(
                 out=y_ps[:],
                 lhsT=h2_codes[g][:, toks].bitcast(FP8X4),
@@ -175,10 +200,13 @@ def tile_gatblock_pb_kernel(
                 start=True,
                 stop=True,
             )
+
+        def add_x1(i):
+            g, s = divmod(i, GROUP)
             x1[i] = work.tile([P, D], F32, tag="x1", bufs=6, name="x1_%d" % i)
             nc.vector.scalar_tensor_tensor(
                 out=x1[i][:],
-                in0=y_ps[:],
+                in0=y[i][:],
                 scalar=1.0,
                 in1=t_sb[i][:],
                 op0=ALU.mult,
@@ -220,24 +248,37 @@ def tile_gatblock_pb_kernel(
                 )
 
         def h_planes_bank(g, first):
-            if first == 0:
-                h_planes[g] = work.tile([P, PACK, TOK], BF16, tag="h_planes", bufs=3, name="h_planes%d" % g)
-            nT_ps = psum.tile([P, PLANES_A_BANK, TOK], F32, tag="bank")
+            nT_ps = psum.tile([P, PLANES_A_BANK, TOK], F32, tag=TAG_N)
+            nT[g, first] = nT_ps
             for j in range(PLANES_A_BANK):
                 t = first + j
                 for s in range(GROUP):
                     nc.tensor.transpose(
                         nT_ps[:, j, s * P : (s + 1) * P], normed[g * GROUP + s][:, t * P : (t + 1) * P], ident_f[:]
                     )
+
+        def empty_planes(g, first):
+            if first == 0:
+                h_planes[g] = work.tile([P, PACK, TOK], BF16, tag="h_planes", bufs=3, name="h_planes%d" % g)
             for j in range(PLANES_A_BANK):
                 t = first + j
-                nc.scalar.activation(
-                    out=h_planes[g][:, t, :],
-                    in_=nT_ps[:, j, :],
-                    func=ACT.Identity,
-                    scale=gb[:, t : t + 1],
-                    bias=gb[:, PACK + t : PACK + t + 1],
-                )
+                if PLANES_ON_V(g, first):
+                    nc.vector.tensor_scalar(
+                        out=h_planes[g][:, t, :],
+                        in0=nT[g, first][:, j, :],
+                        scalar1=gb[:, t : t + 1],
+                        scalar2=gb[:, PACK + t : PACK + t + 1],
+                        op0=ALU.mult,
+                        op1=ALU.add,
+                    )
+                else:
+                    nc.scalar.activation(
+                        out=h_planes[g][:, t, :],
+                        in_=nT[g, first][:, j, :],
+                        func=ACT.Identity,
+                        scale=gb[:, t : t + 1],
+                        bias=gb[:, PACK + t : PACK + t + 1],
+                    )
 
         def regroup_h(g):
             h_grouped[g] = work.tile([P, TOK, PACK], BF16, align_bytes=64, tag="h_grouped", bufs=3, name="h_grouped%d" % g)
@@ -262,7 +303,10 @@ def tile_gatblock_pb_kernel(
         def regroup_w1(j):
             w1_grouped[j] = const.tile([P, BANK, PACK], BF16, align_bytes=64, name="w1_grouped%d" % j)
             dst, src = runs_of_four(w1_planes[j][:], w1_grouped[j][:])
-            nc.vector.tensor_copy(out=dst, in_=src)
+            if W1_ON_G(j):
+                nc.gpsimd.tensor_scalar(out=dst, in0=src, scalar1=1.0, scalar2=0.0, op0=ALU.mult, op1=ALU.add)
+            else:
+                nc.vector.tensor_copy(out=dst, in_=src)
 
         def quantise_w1(j):
             cols = slice(j * BANK, (j + 1) * BANK)
@@ -275,10 +319,10 @@ def tile_gatblock_pb_kernel(
         def stage2(i):
             g, s = divmod(i, GROUP)
             toks = slice(s * P, (s + 1) * P)
-            act[i] = work.tile([P, HID], F32, tag="act", bufs=4, name="act%d" % i)
+            act[i] = work.tile([P, HID], F32, tag="act", bufs=6, name="act%d" % i)
             for j in range(N_BLOCKS):
                 cols = slice(j * BANK, (j + 1) * BANK)
-                o_ps = psum.tile([P, BANK], F32, tag="bank")
+                o_ps = psum.tile([P, BANK], F32, tag=TAG_O)
                 nc.tensor.matmul_mx(
                     out=o_ps[:],
                     lhsT=h_codes[g][:, toks].bitcast(FP8X4),
@@ -290,8 +334,8 @@ def tile_gatblock_pb_kernel(
                 )
                 nc.vector.tensor_tensor(out=act[i][:, cols], in0=o_ps[:], in1=b1_bc[:, cols], op=ALU.add)
 
-        def gelu_and_store(i):
-            for half in range(HID // HALF):
+        def gelu_and_store(i, halves):
+            for half in halves:
                 cols = slice(half * HALF, (half + 1) * HALF)
                 nc.scalar.activation(out=act[i][:, cols], in_=act[i][:, cols], func=ACT.Gelu_apprx_tanh)
                 nc.sync.dma_start(out=out[i][:, cols], in_=act[i][:, cols])
@@ -299,11 +343,12 @@ def tile_gatblock_pb_kernel(
         dst, src = runs_of_four(wx_planes[:], wx_grouped[:])
         nc.vector.tensor_copy(out=dst, in_=src)
         transpose_h2(0)
-        posT_ps = psum.tile([P, P], BF16, tag="bank")
+        empty_h2(0)
+        posT_ps = psum.tile([P, P], BF16, tag=TAG_T)
         nc.tensor.transpose(posT_ps[:], pos_sb[:], ident_b[:])
         posT = const.tile([P, P], BF16)
         nc.vector.tensor_copy(out=posT[:], in_=posT_ps[:])
-        gbT_ps = psum.tile([P, P], BF16, tag="bank")
+        gbT_ps = psum.tile([P, P], BF16, tag=TAG_Y)
         nc.tensor.transpose(gbT_ps[:], gb_rows[:], ident_b[:])
         gb = const.tile([P, 3 * PACK], F32)
         nc.vector.tensor_copy(out=gb[:], in_=gbT_ps[:, 0 : 3 * PACK])
@@ -316,21 +361,24 @@ def tile_gatblock_pb_kernel(
 
         MX_LAG = 1
         SQ_LAG = 2
-        W1_STEP = 3
-        W1_LAG = 3
-        PLANE_LAG = 6
-        OUT_LAG = 11
+        W1_STEP = 1
+        W1_LAG = 2
+        PLANE_LAG = 5
+        OUT_LAG = 8
         for k in range(B + OUT_LAG + 1):
             next_group = k // GROUP + 1
             if k < B:
                 bias_part(k)
                 plain_part(k)
+                empty_t(k)
             if next_group < N_GROUPS and k % GROUP == 0:
                 transpose_h2(next_group)
+                empty_h2(next_group)
             if next_group < N_GROUPS and k % GROUP == GROUP - 1:
                 quantise_h2(next_group)
             if 0 <= k - MX_LAG < B:
                 mx_part(k - MX_LAG)
+                add_x1(k - MX_LAG)
             if 0 <= k - SQ_LAG < B:
                 centred_squares(k - SQ_LAG)
                 if (k - SQ_LAG) % GROUP == GROUP - 1:
@@ -340,6 +388,7 @@ def tile_gatblock_pb_kernel(
             if 0 <= k - PLANE_LAG < B:
                 g, s = divmod(k - PLANE_LAG, GROUP)
                 h_planes_bank(g, s * PLANES_A_BANK)
+                empty_planes(g, s * PLANES_A_BANK)
                 if s == GROUP - 1:
                     regroup_h(g)
             if 0 <= k - W1_STEP - W1_LAG < N_BLOCKS:
@@ -349,4 +398,4 @@ def tile_gatblock_pb_kernel(
             if 0 <= k - OUT_LAG < B:
                 stage2(k - OUT_LAG)
             if 0 <= k - OUT_LAG - 1 < B:
-                gelu_and_store(k - OUT_LAG - 1)
+                gelu_and_store(k - OUT_LAG - 1, [0, 1])

@@ -22,7 +22,8 @@ GROUP = 2
 N_GROUPS = B // GROUP
 TOK = GROUP * P
 PLANES_A_BANK = BANK // TOK
-EARLY_GROUPS = 3
+MID_GROUPS = 3
+EARLY_GROUPS = 2
 HALF = HID // 2
 EPS = 1e-5
 
@@ -43,6 +44,27 @@ def PLANES_ON_V(g, first):
 
 def W1_ON_G(j):
     return False
+
+
+def W1_ON_S(j):
+    return False
+
+
+def NORM_ON_V(g):
+    return g < 3
+
+
+def RG_ON_V(g):
+    return False
+
+
+def NORM_ON_S(g):
+    return False
+
+S_W1 = 128
+S_WX = 256
+SMALL_FIRST = True
+LOADS = "hwx"
 
 
 def runs_of_four(planes, grouped):
@@ -74,30 +96,47 @@ def tile_gatblock_pb_kernel(
         nc.vector.memset(gb_rows[:], 0.0)
 
         wx_planes = const.tile([P, PACK, D], BF16)
-        for u in range(2):
-            nc.sync.dma_start(
-                out=wx_planes[:, 2 * u : 2 * u + 2, :],
-                in_=xfeat_w[256 * u : 256 * (u + 1), :].rearrange("(q e) c -> q e c", e=2),
-            )
-        load_group(h2_sb, h2, 0)
-        load_group(x_sb, x, 0)
-        pos_sb = const.tile([P, P], BF16)
-        nc.scalar.dma_start(out=pos_sb[:], in_=pos_mix)
-        nc.scalar.dma_start(out=gb_rows[0:PACK, :], in_=ln2_g.rearrange("(t p) -> t p", p=P))
-        nc.scalar.dma_start(out=gb_rows[PACK : 2 * PACK, :], in_=ln2_b.rearrange("(t p) -> t p", p=P))
-        nc.scalar.dma_start(out=gb_rows[2 * PACK : 3 * PACK, :], in_=xfeat_b.rearrange("(t p) -> t p", p=P))
+        def load_wx():
+            for u in range(2):
+                nc.sync.dma_start(
+                    out=wx_planes[:, 2 * u : 2 * u + 2, :],
+                    in_=xfeat_w[256 * u : 256 * (u + 1), :].rearrange("(q e) c -> q e c", e=2),
+                )
+        if SMALL_FIRST:
+            pos_sb = const.tile([P, P], BF16)
+            nc.scalar.dma_start(out=pos_sb[:], in_=pos_mix)
+            nc.scalar.dma_start(out=gb_rows[0:PACK, :], in_=ln2_g.rearrange("(t p) -> t p", p=P))
+            nc.scalar.dma_start(out=gb_rows[PACK : 2 * PACK, :], in_=ln2_b.rearrange("(t p) -> t p", p=P))
+            nc.scalar.dma_start(out=gb_rows[2 * PACK : 3 * PACK, :], in_=xfeat_b.rearrange("(t p) -> t p", p=P))
+        for what in LOADS:
+            if what == "w":
+                load_wx()
+            elif what == "h":
+                load_group(h2_sb, h2, 0)
+            else:
+                load_group(x_sb, x, 0)
+        if not SMALL_FIRST:
+            pos_sb = const.tile([P, P], BF16)
+            nc.scalar.dma_start(out=pos_sb[:], in_=pos_mix)
+            nc.scalar.dma_start(out=gb_rows[0:PACK, :], in_=ln2_g.rearrange("(t p) -> t p", p=P))
+            nc.scalar.dma_start(out=gb_rows[PACK : 2 * PACK, :], in_=ln2_b.rearrange("(t p) -> t p", p=P))
+            nc.scalar.dma_start(out=gb_rows[2 * PACK : 3 * PACK, :], in_=xfeat_b.rearrange("(t p) -> t p", p=P))
         for g in range(1, EARLY_GROUPS):
             load_group(h2_sb, h2, g)
             load_group(x_sb, x, g)
         w1_planes = []
         for j in range(N_BLOCKS):
+            if j == N_BLOCKS // 2:
+                for g in range(EARLY_GROUPS, MID_GROUPS):
+                    load_group(h2_sb, h2, g)
+                    load_group(x_sb, x, g)
             w1p = const.tile([P, PACK, BANK], BF16, name="w1_planes%d" % j)
             nc.sync.dma_start(
                 out=w1p[:],
                 in_=mlp_w1[:, j * BANK : (j + 1) * BANK].rearrange("(t p) n -> p t n", p=P),
             )
             w1_planes.append(w1p)
-        for g in range(EARLY_GROUPS, N_GROUPS):
+        for g in range(MID_GROUPS, N_GROUPS):
             load_group(h2_sb, h2, g)
             load_group(x_sb, x, g)
         b1_bc = const.tile([P, HID], BF16)
@@ -117,6 +156,7 @@ def tile_gatblock_pb_kernel(
         neg_mean = [const.tile([P, GROUP], F32, name="neg_mean%d" % g) for g in range(N_GROUPS)]
         sq_sum = [const.tile([P, GROUP], F32, name="sq_sum%d" % g) for g in range(N_GROUPS)]
         var_eps = [const.tile([P, GROUP], F32, name="var_eps%d" % g) for g in range(N_GROUPS)]
+        shift = [const.tile([P, GROUP], F32, name="shift%d" % g) for g in range(N_GROUPS)]
         rstd = [const.tile([P, GROUP], F32, name="rstd%d" % g) for g in range(N_GROUPS)]
 
         wx_grouped = const.tile([P, D, PACK], BF16, align_bytes=64)
@@ -139,7 +179,14 @@ def tile_gatblock_pb_kernel(
         t_sb = [None] * B
         x1 = [None] * B
         normed = [None] * B
-        act = [None] * B
+        act = {}
+
+        def interleave(planes, grouped, width, on_scalar):
+            if on_scalar:
+                dst, src = runs_of_four(planes[:, :, 0:on_scalar], grouped[:, 0:on_scalar, :])
+                nc.scalar.copy(out=dst, in_=src)
+            dst, src = runs_of_four(planes[:, :, on_scalar:width], grouped[:, on_scalar:width, :])
+            nc.vector.tensor_copy(out=dst, in_=src)
 
         def transpose_h2(g):
             h2T_ps = psum.tile([P, 2, TOK], F32, tag=TAG_H2)
@@ -235,10 +282,18 @@ def tile_gatblock_pb_kernel(
                 out=var_eps[g][:], in0=sq_sum[g][:], scalar1=1.0 / (D * D * D), scalar2=EPS, op0=ALU.mult, op1=ALU.add
             )
             nc.gpsimd.tensor_tensor(out=rstd[g][:], in0=var_eps[g][:], in1=neg_half[:], op=ALU.pow)
+            if NORM_ON_S(g):
+                nc.gpsimd.tensor_tensor(out=shift[g][:], in0=neg_mean[g][:], in1=rstd[g][:], op=ALU.mult)
             for s in range(GROUP):
                 i = g * GROUP + s
                 normed[i] = work.tile([P, D], F32, tag="normed", bufs=8, name="normed%d" % i)
-                nc.gpsimd.tensor_scalar(
+                if NORM_ON_S(g):
+                    nc.scalar.activation(
+                        out=normed[i][:], in_=x1[i][:], func=ACT.Identity,
+                        scale=rstd[g][:, s : s + 1], bias=shift[g][:, s : s + 1],
+                    )
+                    continue
+                (nc.vector if NORM_ON_V(g) else nc.gpsimd).tensor_scalar(
                     out=normed[i][:],
                     in0=x1[i][:],
                     scalar1=neg_mean[g][:, s : s + 1],
@@ -282,14 +337,17 @@ def tile_gatblock_pb_kernel(
 
         def regroup_h(g):
             h_grouped[g] = work.tile([P, TOK, PACK], BF16, align_bytes=64, tag="h_grouped", bufs=3, name="h_grouped%d" % g)
-            nc.gpsimd.tensor_scalar(
-                out=h_grouped[g][:],
-                in0=h_planes[g][:].rearrange("p t c -> p c t"),
-                scalar1=1.0,
-                scalar2=0.0,
-                op0=ALU.mult,
-                op1=ALU.add,
-            )
+            if RG_ON_V(g):
+                nc.vector.tensor_copy(out=h_grouped[g][:], in_=h_planes[g][:].rearrange("p t c -> p c t"))
+            else:
+                nc.gpsimd.tensor_scalar(
+                    out=h_grouped[g][:],
+                    in0=h_planes[g][:].rearrange("p t c -> p c t"),
+                    scalar1=1.0,
+                    scalar2=0.0,
+                    op0=ALU.mult,
+                    op1=ALU.add,
+                )
 
         def quantise_h(g):
             h_codes[g] = work.tile([P, TOK], U32, align_bytes=64, tag="h_codes", bufs=3, name="h_codes%d" % g)
@@ -302,11 +360,7 @@ def tile_gatblock_pb_kernel(
 
         def regroup_w1(j):
             w1_grouped[j] = const.tile([P, BANK, PACK], BF16, align_bytes=64, name="w1_grouped%d" % j)
-            dst, src = runs_of_four(w1_planes[j][:], w1_grouped[j][:])
-            if W1_ON_G(j):
-                nc.gpsimd.tensor_scalar(out=dst, in0=src, scalar1=1.0, scalar2=0.0, op0=ALU.mult, op1=ALU.add)
-            else:
-                nc.vector.tensor_copy(out=dst, in_=src)
+            interleave(w1_planes[j], w1_grouped[j], BANK, S_W1)
 
         def quantise_w1(j):
             cols = slice(j * BANK, (j + 1) * BANK)
@@ -316,12 +370,12 @@ def tile_gatblock_pb_kernel(
                 in_=w1_grouped[j][:].rearrange("p c t -> p (c t)"),
             )
 
-        def stage2(i):
+        def stage2(i, half):
             g, s = divmod(i, GROUP)
             toks = slice(s * P, (s + 1) * P)
-            act[i] = work.tile([P, HID], F32, tag="act", bufs=6, name="act%d" % i)
-            for j in range(N_BLOCKS):
-                cols = slice(j * BANK, (j + 1) * BANK)
+            act[i, half] = work.tile([P, HALF], F32, tag="act", bufs=12, name="act%d_%d" % (i, half))
+            for j in range(HALF // BANK):
+                cols = slice(half * HALF + j * BANK, half * HALF + (j + 1) * BANK)
                 o_ps = psum.tile([P, BANK], F32, tag=TAG_O)
                 nc.tensor.matmul_mx(
                     out=o_ps[:],
@@ -332,18 +386,17 @@ def tile_gatblock_pb_kernel(
                     start=True,
                     stop=True,
                 )
-                nc.vector.tensor_tensor(out=act[i][:, cols], in0=o_ps[:], in1=b1_bc[:, cols], op=ALU.add)
+                nc.vector.tensor_tensor(
+                    out=act[i, half][:, j * BANK : (j + 1) * BANK], in0=o_ps[:], in1=b1_bc[:, cols], op=ALU.add
+                )
 
-        def gelu_and_store(i, halves):
-            for half in halves:
-                cols = slice(half * HALF, (half + 1) * HALF)
-                nc.scalar.activation(out=act[i][:, cols], in_=act[i][:, cols], func=ACT.Gelu_apprx_tanh)
-                nc.sync.dma_start(out=out[i][:, cols], in_=act[i][:, cols])
+        def gelu_and_store(i, half, pieces=1):
+            width = HALF // pieces
+            for q in range(pieces):
+                cols = slice(q * width, (q + 1) * width)
+                nc.scalar.activation(out=act[i, half][:, cols], in_=act[i, half][:, cols], func=ACT.Gelu_apprx_tanh)
+                nc.sync.dma_start(out=out[i][:, half * HALF + q * width : half * HALF + (q + 1) * width], in_=act[i, half][:, cols])
 
-        dst, src = runs_of_four(wx_planes[:], wx_grouped[:])
-        nc.vector.tensor_copy(out=dst, in_=src)
-        transpose_h2(0)
-        empty_h2(0)
         posT_ps = psum.tile([P, P], BF16, tag=TAG_T)
         nc.tensor.transpose(posT_ps[:], pos_sb[:], ident_b[:])
         posT = const.tile([P, P], BF16)
@@ -352,6 +405,9 @@ def tile_gatblock_pb_kernel(
         nc.tensor.transpose(gbT_ps[:], gb_rows[:], ident_b[:])
         gb = const.tile([P, 3 * PACK], F32)
         nc.vector.tensor_copy(out=gb[:], in_=gbT_ps[:, 0 : 3 * PACK])
+        transpose_h2(0)
+        empty_h2(0)
+        interleave(wx_planes, wx_grouped, D, S_WX)
         nc.vector.quantize_mx(
             out=wx_codes[:].bitcast(FP8X4),
             scales=wx_scales[:],
@@ -361,10 +417,12 @@ def tile_gatblock_pb_kernel(
 
         MX_LAG = 1
         SQ_LAG = 2
-        W1_STEP = 1
-        W1_LAG = 2
+        W1_STEP = 0
+        W1_GAP = 1
+        W1_LAG = 1
         PLANE_LAG = 5
-        OUT_LAG = 8
+        OUT_LAG = 9
+        w1_steps = [W1_STEP + j + (W1_GAP if 2 * j >= N_BLOCKS else 0) for j in range(N_BLOCKS)]
         for k in range(B + OUT_LAG + 1):
             next_group = k // GROUP + 1
             if k < B:
@@ -383,19 +441,25 @@ def tile_gatblock_pb_kernel(
                 centred_squares(k - SQ_LAG)
                 if (k - SQ_LAG) % GROUP == GROUP - 1:
                     normalise((k - SQ_LAG) // GROUP)
-            if 0 <= k - W1_STEP < N_BLOCKS:
-                regroup_w1(k - W1_STEP)
+            for j in range(N_BLOCKS):
+                if k == w1_steps[j]:
+                    regroup_w1(j)
             if 0 <= k - PLANE_LAG < B:
                 g, s = divmod(k - PLANE_LAG, GROUP)
                 h_planes_bank(g, s * PLANES_A_BANK)
                 empty_planes(g, s * PLANES_A_BANK)
                 if s == GROUP - 1:
                     regroup_h(g)
-            if 0 <= k - W1_STEP - W1_LAG < N_BLOCKS:
-                quantise_w1(k - W1_STEP - W1_LAG)
+            for j in range(N_BLOCKS):
+                if k == w1_steps[j] + W1_LAG:
+                    quantise_w1(j)
             if 0 <= k - OUT_LAG + 1 < B and (k - OUT_LAG + 1) % GROUP == 0:
                 quantise_h((k - OUT_LAG + 1) // GROUP)
             if 0 <= k - OUT_LAG < B:
-                stage2(k - OUT_LAG)
+                g, half = divmod(k - OUT_LAG, GROUP)
+                for s in range(GROUP):
+                    stage2(g * GROUP + s, half)
             if 0 <= k - OUT_LAG - 1 < B:
-                gelu_and_store(k - OUT_LAG - 1, [0, 1])
+                g, half = divmod(k - OUT_LAG - 1, GROUP)
+                for s in range(GROUP):
+                    gelu_and_store(g * GROUP + s, half, 2 if g == N_GROUPS - 1 and half == 1 and s == GROUP - 1 else 1)

@@ -63,6 +63,7 @@ def NORM_ON_S(g):
 
 S_W1 = 128
 S_WX = 256
+PRE_W1 = False
 SMALL_FIRST = True
 LOADS = "hwx"
 
@@ -108,9 +109,19 @@ def tile_gatblock_pb_kernel(
             nc.scalar.dma_start(out=gb_rows[0:PACK, :], in_=ln2_g.rearrange("(t p) -> t p", p=P))
             nc.scalar.dma_start(out=gb_rows[PACK : 2 * PACK, :], in_=ln2_b.rearrange("(t p) -> t p", p=P))
             nc.scalar.dma_start(out=gb_rows[2 * PACK : 3 * PACK, :], in_=xfeat_b.rearrange("(t p) -> t p", p=P))
+        w1_planes = [None] * N_BLOCKS
+        def load_w1(j):
+            w1p = const.tile([P, PACK, BANK], BF16, name="w1_planes%d" % j)
+            nc.sync.dma_start(
+                out=w1p[:],
+                in_=mlp_w1[:, j * BANK : (j + 1) * BANK].rearrange("(t p) n -> p t n", p=P),
+            )
+            w1_planes[j] = w1p
         for what in LOADS:
             if what == "w":
                 load_wx()
+            elif what in "0123":
+                load_w1(int(what))
             elif what == "h":
                 load_group(h2_sb, h2, 0)
             else:
@@ -124,18 +135,13 @@ def tile_gatblock_pb_kernel(
         for g in range(1, EARLY_GROUPS):
             load_group(h2_sb, h2, g)
             load_group(x_sb, x, g)
-        w1_planes = []
         for j in range(N_BLOCKS):
             if j == N_BLOCKS // 2:
                 for g in range(EARLY_GROUPS, MID_GROUPS):
                     load_group(h2_sb, h2, g)
                     load_group(x_sb, x, g)
-            w1p = const.tile([P, PACK, BANK], BF16, name="w1_planes%d" % j)
-            nc.sync.dma_start(
-                out=w1p[:],
-                in_=mlp_w1[:, j * BANK : (j + 1) * BANK].rearrange("(t p) n -> p t n", p=P),
-            )
-            w1_planes.append(w1p)
+            if w1_planes[j] is None:
+                load_w1(j)
         for g in range(MID_GROUPS, N_GROUPS):
             load_group(h2_sb, h2, g)
             load_group(x_sb, x, g)
@@ -284,6 +290,8 @@ def tile_gatblock_pb_kernel(
             nc.gpsimd.tensor_tensor(out=rstd[g][:], in0=var_eps[g][:], in1=neg_half[:], op=ALU.pow)
             if NORM_ON_S(g):
                 nc.gpsimd.tensor_tensor(out=shift[g][:], in0=neg_mean[g][:], in1=rstd[g][:], op=ALU.mult)
+
+        def norm_rows(g):
             for s in range(GROUP):
                 i = g * GROUP + s
                 normed[i] = work.tile([P, D], F32, tag="normed", bufs=8, name="normed%d" % i)
@@ -360,7 +368,11 @@ def tile_gatblock_pb_kernel(
 
         def regroup_w1(j):
             w1_grouped[j] = const.tile([P, BANK, PACK], BF16, align_bytes=64, name="w1_grouped%d" % j)
-            interleave(w1_planes[j], w1_grouped[j], BANK, S_W1)
+            if W1_ON_G(j):
+                dst, src = runs_of_four(w1_planes[j][:], w1_grouped[j][:])
+                nc.gpsimd.tensor_scalar(out=dst, in0=src, scalar1=1.0, scalar2=0.0, op0=ALU.mult, op1=ALU.add)
+            else:
+                interleave(w1_planes[j], w1_grouped[j], BANK, S_W1)
 
         def quantise_w1(j):
             cols = slice(j * BANK, (j + 1) * BANK)
@@ -407,6 +419,8 @@ def tile_gatblock_pb_kernel(
         nc.vector.tensor_copy(out=gb[:], in_=gbT_ps[:, 0 : 3 * PACK])
         transpose_h2(0)
         empty_h2(0)
+        if PRE_W1:
+            regroup_w1(0)
         interleave(wx_planes, wx_grouped, D, S_WX)
         nc.vector.quantize_mx(
             out=wx_codes[:].bitcast(FP8X4),
@@ -414,16 +428,21 @@ def tile_gatblock_pb_kernel(
             in_=wx_grouped[:].rearrange("p c t -> p (c t)"),
         )
         quantise_h2(0)
+        if PRE_W1:
+            quantise_w1(0)
 
         MX_LAG = 1
         SQ_LAG = 2
         W1_STEP = 0
         W1_GAP = 1
         W1_LAG = 1
-        PLANE_LAG = 5
-        OUT_LAG = 9
+        NORM_LAG = 3
+        NORM_POS = 1
+        PLANE_LAG = 6
+        OUT_LAG = 10
+        GELU_LAG = 1
         w1_steps = [W1_STEP + j + (W1_GAP if 2 * j >= N_BLOCKS else 0) for j in range(N_BLOCKS)]
-        for k in range(B + OUT_LAG + 1):
+        for k in range(B + OUT_LAG + GELU_LAG):
             next_group = k // GROUP + 1
             if k < B:
                 bias_part(k)
@@ -441,9 +460,15 @@ def tile_gatblock_pb_kernel(
                 centred_squares(k - SQ_LAG)
                 if (k - SQ_LAG) % GROUP == GROUP - 1:
                     normalise((k - SQ_LAG) // GROUP)
+                    if not NORM_ON_V((k - SQ_LAG) // GROUP):
+                        norm_rows((k - SQ_LAG) // GROUP)
+            if NORM_POS == 0 and 0 <= k - NORM_LAG < B and (k - NORM_LAG) % GROUP == GROUP - 1 and NORM_ON_V((k - NORM_LAG) // GROUP):
+                norm_rows((k - NORM_LAG) // GROUP)
             for j in range(N_BLOCKS):
-                if k == w1_steps[j]:
+                if k == w1_steps[j] and not (PRE_W1 and j == 0):
                     regroup_w1(j)
+            if NORM_POS == 1 and 0 <= k - NORM_LAG < B and (k - NORM_LAG) % GROUP == GROUP - 1 and NORM_ON_V((k - NORM_LAG) // GROUP):
+                norm_rows((k - NORM_LAG) // GROUP)
             if 0 <= k - PLANE_LAG < B:
                 g, s = divmod(k - PLANE_LAG, GROUP)
                 h_planes_bank(g, s * PLANES_A_BANK)
@@ -451,7 +476,7 @@ def tile_gatblock_pb_kernel(
                 if s == GROUP - 1:
                     regroup_h(g)
             for j in range(N_BLOCKS):
-                if k == w1_steps[j] + W1_LAG:
+                if k == w1_steps[j] + W1_LAG and not (PRE_W1 and j == 0):
                     quantise_w1(j)
             if 0 <= k - OUT_LAG + 1 < B and (k - OUT_LAG + 1) % GROUP == 0:
                 quantise_h((k - OUT_LAG + 1) // GROUP)
@@ -459,7 +484,9 @@ def tile_gatblock_pb_kernel(
                 g, half = divmod(k - OUT_LAG, GROUP)
                 for s in range(GROUP):
                     stage2(g * GROUP + s, half)
-            if 0 <= k - OUT_LAG - 1 < B:
-                g, half = divmod(k - OUT_LAG - 1, GROUP)
+            if 0 <= k - OUT_LAG - GELU_LAG < B:
+                g, half = divmod(k - OUT_LAG - GELU_LAG, GROUP)
                 for s in range(GROUP):
                     gelu_and_store(g * GROUP + s, half, 2 if g == N_GROUPS - 1 and half == 1 and s == GROUP - 1 else 1)
+            if NORM_POS == 2 and 0 <= k - NORM_LAG < B and (k - NORM_LAG) % GROUP == GROUP - 1 and NORM_ON_V((k - NORM_LAG) // GROUP):
+                norm_rows((k - NORM_LAG) // GROUP)

@@ -22,8 +22,8 @@ GROUP = 2
 N_GROUPS = B // GROUP
 TOK = GROUP * P
 PLANES_A_BANK = BANK // TOK
-MID_GROUPS = 3
-EARLY_GROUPS = 2
+MID_GROUPS = 4
+EARLY_GROUPS = 4
 HALF = HID // 2
 EPS = 1e-5
 
@@ -62,10 +62,11 @@ def NORM_ON_S(g):
     return False
 
 S_W1 = 128
-S_WX = 256
+S_WX = 128
 PRE_W1 = False
+HQ_FIRST = False
 SMALL_FIRST = True
-LOADS = "hwx"
+LOADS = "hwx1ab2cd345"
 
 
 def runs_of_four(planes, grouped):
@@ -120,8 +121,11 @@ def tile_gatblock_pb_kernel(
         for what in LOADS:
             if what == "w":
                 load_wx()
-            elif what in "0123":
-                load_w1(int(what))
+            elif what in "abcd":
+                load_w1("abcd".index(what))
+            elif what in "12345":
+                load_group(h2_sb, h2, int(what))
+                load_group(x_sb, x, int(what))
             elif what == "h":
                 load_group(h2_sb, h2, 0)
             else:
@@ -132,19 +136,6 @@ def tile_gatblock_pb_kernel(
             nc.scalar.dma_start(out=gb_rows[0:PACK, :], in_=ln2_g.rearrange("(t p) -> t p", p=P))
             nc.scalar.dma_start(out=gb_rows[PACK : 2 * PACK, :], in_=ln2_b.rearrange("(t p) -> t p", p=P))
             nc.scalar.dma_start(out=gb_rows[2 * PACK : 3 * PACK, :], in_=xfeat_b.rearrange("(t p) -> t p", p=P))
-        for g in range(1, EARLY_GROUPS):
-            load_group(h2_sb, h2, g)
-            load_group(x_sb, x, g)
-        for j in range(N_BLOCKS):
-            if j == N_BLOCKS // 2:
-                for g in range(EARLY_GROUPS, MID_GROUPS):
-                    load_group(h2_sb, h2, g)
-                    load_group(x_sb, x, g)
-            if w1_planes[j] is None:
-                load_w1(j)
-        for g in range(MID_GROUPS, N_GROUPS):
-            load_group(h2_sb, h2, g)
-            load_group(x_sb, x, g)
         b1_bc = const.tile([P, HID], BF16)
         nc.sync.dma_start(out=b1_bc[:], in_=mlp_b1.partition_broadcast(P))
 
@@ -422,20 +413,25 @@ def tile_gatblock_pb_kernel(
         if PRE_W1:
             regroup_w1(0)
         interleave(wx_planes, wx_grouped, D, S_WX)
+        if HQ_FIRST:
+            quantise_h2(0)
         nc.vector.quantize_mx(
             out=wx_codes[:].bitcast(FP8X4),
             scales=wx_scales[:],
             in_=wx_grouped[:].rearrange("p c t -> p (c t)"),
         )
-        quantise_h2(0)
+        if not HQ_FIRST:
+            quantise_h2(0)
         if PRE_W1:
             quantise_w1(0)
 
+        H2_ODD = 0
+        Q2_POS = 1
         MX_LAG = 1
         SQ_LAG = 2
         W1_STEP = 0
         W1_GAP = 1
-        W1_LAG = 1
+        W1_LAG = 2
         NORM_LAG = 3
         NORM_POS = 1
         PLANE_LAG = 6
@@ -448,14 +444,16 @@ def tile_gatblock_pb_kernel(
                 bias_part(k)
                 plain_part(k)
                 empty_t(k)
-            if next_group < N_GROUPS and k % GROUP == 0:
+            if next_group < N_GROUPS and k % GROUP == H2_ODD:
                 transpose_h2(next_group)
                 empty_h2(next_group)
-            if next_group < N_GROUPS and k % GROUP == GROUP - 1:
+            if Q2_POS == 0 and next_group < N_GROUPS and k % GROUP == GROUP - 1:
                 quantise_h2(next_group)
             if 0 <= k - MX_LAG < B:
                 mx_part(k - MX_LAG)
                 add_x1(k - MX_LAG)
+            if Q2_POS == 1 and next_group < N_GROUPS and k % GROUP == GROUP - 1:
+                quantise_h2(next_group)
             if 0 <= k - SQ_LAG < B:
                 centred_squares(k - SQ_LAG)
                 if (k - SQ_LAG) % GROUP == GROUP - 1:

@@ -66,7 +66,7 @@ S_WX = 128
 PRE_W1 = False
 HQ_FIRST = False
 SMALL_FIRST = True
-LOADS = "hwx1ab2cd345"
+LOADS = "hwx1ab23cd45"
 
 
 def runs_of_four(planes, grouped):
@@ -485,6 +485,6 @@ def tile_gatblock_pb_kernel(
             if 0 <= k - OUT_LAG - GELU_LAG < B:
                 g, half = divmod(k - OUT_LAG - GELU_LAG, GROUP)
                 for s in range(GROUP):
-                    gelu_and_store(g * GROUP + s, half, 2 if g == N_GROUPS - 1 and half == 1 and s == GROUP - 1 else 1)
+                    gelu_and_store(g * GROUP + s, half)
             if NORM_POS == 2 and 0 <= k - NORM_LAG < B and (k - NORM_LAG) % GROUP == GROUP - 1 and NORM_ON_V((k - NORM_LAG) // GROUP):
                 norm_rows((k - NORM_LAG) // GROUP)

from contextlib import ExitStack

import concourse.mybir as mybir
from concourse.masks import make_identity

F32 = mybir.dt.float32
BF16 = mybir.dt.bfloat16
U32 = mybir.dt.uint32
U8 = mybir.dt.uint8
FP8X4 = mybir.dt.float8_e4m3fn_x4
ACT = mybir.ActivationFunctionType
ALU = mybir.AluOpType

P = 128
PACK = 4
B = 12
D = 512
HID = 2048
BANK = 512
N_BLOCKS = HID // BANK
GROUP = 2
N_GROUPS = B // GROUP
TOK = GROUP * P
PLANES_A_BANK = BANK // TOK
MID_GROUPS = 4
EARLY_GROUPS = 4
HALF = HID // 2
EPS = 1e-5

FLOPS = 2 * B * P * (D * D + D * HID + P * D)


TAG_H2 = TAG_T = TAG_Y = TAG_N = TAG_O = "bank"
PSUM_BUFS = 8


def H2_ON_V(g):
    return False


def PLANES_ON_V(g, first):
    return g > 1 and first > 0


def W1_ON_G(j):
    return False


def W1_ON_S(j):
    return False


def NORM_ON_V(g):
    return g < 3


def RG_ON_V(g):
    return False


def NORM_ON_S(g):
    return False

S_W1 = 128
S_WX = 128
PRE_W1 = False
HQ_FIRST = False
SMALL_FIRST = True
LOADS = "hwx1ab23cd45"


def runs_of_four(planes, grouped):
    return (
        grouped.rearrange("p (c i) t -> p c t i", i=4),
        planes.rearrange("p t (c i) -> p c t i", i=4),
    )


def tile_gatblock_pb_kernel(
    tc, x, h2, xfeat_w, xfeat_b, pos_mix, ln2_g, ln2_b, mlp_w1, mlp_b1, out
):
    nc = tc.nc
    with ExitStack() as stack:
        const = stack.enter_context(tc.tile_pool(name="const", bufs=1))
        work = stack.enter_context(tc.tile_pool(name="work", bufs=2))
        psum = stack.enter_context(tc.psum_pool(name="psum", bufs=PSUM_BUFS))
        stack.enter_context(tc.manual_schedule())

        h2_sb = [const.tile([P, GROUP, D], BF16, name="h2_sb%d" % g) for g in range(N_GROUPS)]
        x_sb = [const.tile([P, GROUP, D], BF16, name="x_sb%d" % g) for g in range(N_GROUPS)]

        def load_group(dst, src, g):
            nc.sync.dma_start(
                out=dst[g][:], in_=src[g * GROUP : (g + 1) * GROUP].rearrange("b n d -> n b d")
            )

        gb_rows = const.tile([P, P], BF16)
        nc.vector.memset(gb_rows[:], 0.0)

        wx_planes = const.tile([P, PACK, D], BF16)
        def load_wx():
            for u in range(2):
                nc.sync.dma_start(
                    out=wx_planes[:, 2 * u : 2 * u + 2, :],
                    in_=xfeat_w[256 * u : 256 * (u + 1), :].rearrange("(q e) c -> q e c", e=2),
                )
        if SMALL_FIRST:
            pos_sb = const.tile([P, P], BF16)
            nc.scalar.dma_start(out=pos_sb[:], in_=pos_mix)
            nc.scalar.dma_start(out=gb_rows[0:PACK, :], in_=ln2_g.rearrange("(t p) -> t p", p=P))
            nc.scalar.dma_start(out=gb_rows[PACK : 2 * PACK, :], in_=ln2_b.rearrange("(t p) -> t p", p=P))
            nc.scalar.dma_start(out=gb_rows[2 * PACK : 3 * PACK, :], in_=xfeat_b.rearrange("(t p) -> t p", p=P))
        w1_planes = [None] * N_BLOCKS
        def load_w1(j):
            w1p = const.tile([P, PACK, BANK], BF16, name="w1_planes%d" % j)
            nc.sync.dma_start(
                out=w1p[:],
                in_=mlp_w1[:, j * BANK : (j + 1) * BANK].rearrange("(t p) n -> p t n", p=P),
            )
            w1_planes[j] = w1p
        for what in LOADS:
            if what == "w":
                load_wx()
            elif what in "abcd":
                load_w1("abcd".index(what))
            elif what in "12345":
                load_group(h2_sb, h2, int(what))
                load_group(x_sb, x, int(what))
            elif what == "h":
                load_group(h2_sb, h2, 0)
            else:
                load_group(x_sb, x, 0)
        if not SMALL_FIRST:
            pos_sb = const.tile([P, P], BF16)
            nc.scalar.dma_start(out=pos_sb[:], in_=pos_mix)
            nc.scalar.dma_start(out=gb_rows[0:PACK, :], in_=ln2_g.rearrange("(t p) -> t p", p=P))
            nc.scalar.dma_start(out=gb_rows[PACK : 2 * PACK, :], in_=ln2_b.rearrange("(t p) -> t p", p=P))
            nc.scalar.dma_start(out=gb_rows[2 * PACK : 3 * PACK, :], in_=xfeat_b.rearrange("(t p) -> t p", p=P))
        b1_bc = const.tile([P, HID], BF16)
        nc.sync.dma_start(out=b1_bc[:], in_=mlp_b1.partition_broadcast(P))

        warm = const.tile([P, 1], F32)
        nc.vector.memset(warm[:], 0.0)
        nc.scalar.activation(out=warm[:], in_=warm[:], func=ACT.Gelu_apprx_tanh)
        neg_half = const.tile([P, GROUP], F32)
        nc.vector.memset(neg_half[:], -0.5)
        ident_f = const.tile([P, P], F32)
        make_identity(nc, ident_f[:])
        ident_b = const.tile([P, P], BF16)
        make_identity(nc, ident_b[:])

        row_sum = [const.tile([P, GROUP], F32, name="row_sum%d" % g) for g in range(N_GROUPS)]
        neg_mean = [const.tile([P, GROUP], F32, name="neg_mean%d" % g) for g in range(N_GROUPS)]
        sq_sum = [const.tile([P, GROUP], F32, name="sq_sum%d" % g) for g in range(N_GROUPS)]
        var_eps = [const.tile([P, GROUP], F32, name="var_eps%d" % g) for g in range(N_GROUPS)]
        shift = [const.tile([P, GROUP], F32, name="shift%d" % g) for g in range(N_GROUPS)]
        rstd = [const.tile([P, GROUP], F32, name="rstd%d" % g) for g in range(N_GROUPS)]

        wx_grouped = const.tile([P, D, PACK], BF16, align_bytes=64)
        wx_codes = const.tile([P, D], U32, align_bytes=64)
        wx_scales = const.tile([P, D], U8, align_bytes=64)
        w1_codes = const.tile([P, HID], U32, align_bytes=64)
        w1_scales = const.tile([P, HID], U8, align_bytes=64)
        w1_grouped = [None] * N_BLOCKS
        h2_grouped = [None] * N_GROUPS
        h2_codes = [None] * N_GROUPS
        h2_scales = [None] * N_GROUPS
        h_planes = [None] * N_GROUPS
        h_grouped = [None] * N_GROUPS
        h_codes = [None] * N_GROUPS
        h_scales = [None] * N_GROUPS
        t_ps = [None] * B
        y = [None] * B
        h2T = [None] * N_GROUPS
        nT = {}
        t_sb = [None] * B
        x1 = [None] * B
        normed = [None] * B
        act = {}

        def interleave(planes, grouped, width, on_scalar):
            if on_scalar:
                dst, src = runs_of_four(planes[:, :, 0:on_scalar], grouped[:, 0:on_scalar, :])
                nc.scalar.copy(out=dst, in_=src)
            dst, src = runs_of_four(planes[:, :, on_scalar:width], grouped[:, on_scalar:width, :])
            nc.vector.tensor_copy(out=dst, in_=src)

        def transpose_h2(g):
            h2T_ps = psum.tile([P, 2, TOK], F32, tag=TAG_H2)
            h2T[g] = h2T_ps
            for s in range(GROUP):
                h2_words = h2_sb[g][:, s, :].bitcast(F32)
                for u in range(2):
                    nc.tensor.transpose(
                        h2T_ps[:, u, s * P : (s + 1) * P], h2_words[:, u * P : (u + 1) * P], ident_f[:]
                    )

        def empty_h2(g):
            h2_grouped[g] = work.tile([P, TOK * PACK], BF16, align_bytes=64, tag="h2g", bufs=3, name="h2g%d" % g)
            (nc.vector.tensor_copy if H2_ON_V(g) else nc.scalar.copy)(
                out=h2_grouped[g][:].bitcast(F32).rearrange("p (n u) -> p n u", u=2),
                in_=h2T[g][:].rearrange("p u n -> p n u"),
            )

        def quantise_h2(g):
            h2_codes[g] = work.tile([P, TOK], U32, align_bytes=64, tag="h2c", bufs=3, name="h2c%d" % g)
            h2_scales[g] = work.tile([P, TOK], U8, align_bytes=64, tag="h2s", bufs=3, name="h2s%d" % g)
            nc.vector.quantize_mx(
                out=h2_codes[g][:].bitcast(FP8X4), scales=h2_scales[g][:], in_=h2_grouped[g][:]
            )

        def bias_part(i):
            t_ps[i] = psum.tile([P, D], F32, tag=TAG_T, name="t_ps%d" % i)
            for c in range(PACK):
                nc.tensor.matmul(
                    t_ps[i][:, c * P : (c + 1) * P],
                    lhsT=gb[:, 2 * PACK + c : 2 * PACK + c + 1].to_broadcast([P, P]),
                    rhs=ident_f[:],
                    is_transpose=True,
                    start=(c == 0),
                    stop=False,
                )

        def plain_part(i):
            g, s = divmod(i, GROUP)
            nc.tensor.matmul(t_ps[i][:], lhsT=posT[:], rhs=h2_sb[g][:, s, :], start=False, stop=False)
            nc.tensor.matmul(t_ps[i][:], lhsT=ident_b[:], rhs=x_sb[g][:, s, :], start=False, stop=True)

        def empty_t(i):
            t_sb[i] = work.tile([P, D], F32, tag="t_sb", bufs=3, name="t_sb%d" % i)
            nc.scalar.copy(out=t_sb[i][:], in_=t_ps[i][:])

        def mx_part(i):
            g, s = divmod(i, GROUP)
            toks = slice(s * P, (s + 1) * P)
            y_ps = psum.tile([P, D], F32, tag=TAG_Y)
            y[i] = y_ps
            nc.tensor.matmul_mx(
                out=y_ps[:],
                lhsT=h2_codes[g][:, toks].bitcast(FP8X4),
                lhsT_scale=h2_scales[g][:, toks],
                rhs=wx_codes[:].bitcast(FP8X4),
                rhs_scale=wx_scales[:],
                start=True,
                stop=True,
            )

        def add_x1(i):
            g, s = divmod(i, GROUP)
            x1[i] = work.tile([P, D], F32, tag="x1", bufs=6, name="x1_%d" % i)
            nc.vector.scalar_tensor_tensor(
                out=x1[i][:],
                in0=y[i][:],
                scalar=1.0,
                in1=t_sb[i][:],
                op0=ALU.mult,
                op1=ALU.add,
                accum_out=row_sum[g][:, s : s + 1],
            )

        def centred_squares(i):
            g, s = divmod(i, GROUP)
            col = slice(s, s + 1)
            squares = work.tile([P, D], BF16, tag="squares", bufs=4)
            nc.scalar.activation(
                out=squares[:],
                in_=x1[i][:],
                func=ACT.Square,
                bias=row_sum[g][:, col],
                scale=-1.0 * D,
                accum_out=sq_sum[g][:, col],
            )

        def normalise(g):
            nc.gpsimd.tensor_scalar(
                out=neg_mean[g][:], in0=row_sum[g][:], scalar1=-1.0 / D, scalar2=0.0, op0=ALU.mult, op1=ALU.add
            )
            nc.gpsimd.tensor_scalar(
                out=var_eps[g][:], in0=sq_sum[g][:], scalar1=1.0 / (D * D * D), scalar2=EPS, op0=ALU.mult, op1=ALU.add
            )
            nc.gpsimd.tensor_tensor(out=rstd[g][:], in0=var_eps[g][:], in1=neg_half[:], op=ALU.pow)
            if NORM_ON_S(g):
                nc.gpsimd.tensor_tensor(out=shift[g][:], in0=neg_mean[g][:], in1=rstd[g][:], op=ALU.mult)

        def norm_rows(g):
            for s in range(GROUP):
                i = g * GROUP + s
                normed[i] = work.tile([P, D], F32, tag="normed", bufs=8, name="normed%d" % i)
                if NORM_ON_S(g):
                    nc.scalar.activation(
                        out=normed[i][:], in_=x1[i][:], func=ACT.Identity,
                        scale=rstd[g][:, s : s + 1], bias=shift[g][:, s : s + 1],
                    )
                    continue
                (nc.vector if NORM_ON_V(g) else nc.gpsimd).tensor_scalar(
                    out=normed[i][:],
                    in0=x1[i][:],
                    scalar1=neg_mean[g][:, s : s + 1],
                    scalar2=rstd[g][:, s : s + 1],
                    op0=ALU.add,
                    op1=ALU.mult,
                )

        def h_planes_bank(g, first):
            nT_ps = psum.tile([P, PLANES_A_BANK, TOK], F32, tag=TAG_N)
            nT[g, first] = nT_ps
            for j in range(PLANES_A_BANK):
                t = first + j
                for s in range(GROUP):
                    nc.tensor.transpose(
                        nT_ps[:, j, s * P : (s + 1) * P], normed[g * GROUP + s][:, t * P : (t + 1) * P], ident_f[:]
                    )

        def empty_planes(g, first):
            if first == 0:
                h_planes[g] = work.tile([P, PACK, TOK], BF16, tag="h_planes", bufs=3, name="h_planes%d" % g)
            for j in range(PLANES_A_BANK):
                t = first + j
                if PLANES_ON_V(g, first):
                    nc.vector.tensor_scalar(
                        out=h_planes[g][:, t, :],
                        in0=nT[g, first][:, j, :],
                        scalar1=gb[:, t : t + 1],
                        scalar2=gb[:, PACK + t : PACK + t + 1],
                        op0=ALU.mult,
                        op1=ALU.add,
                    )
                else:
                    nc.scalar.activation(
                        out=h_planes[g][:, t, :],
                        in_=nT[g, first][:, j, :],
                        func=ACT.Identity,
                        scale=gb[:, t : t + 1],
                        bias=gb[:, PACK + t : PACK + t + 1],
                    )

        def regroup_h(g):
            h_grouped[g] = work.tile([P, TOK, PACK], BF16, align_bytes=64, tag="h_grouped", bufs=3, name="h_grouped%d" % g)
            if RG_ON_V(g):
                nc.vector.tensor_copy(out=h_grouped[g][:], in_=h_planes[g][:].rearrange("p t c -> p c t"))
            else:
                nc.gpsimd.tensor_scalar(
                    out=h_grouped[g][:],
                    in0=h_planes[g][:].rearrange("p t c -> p c t"),
                    scalar1=1.0,
                    scalar2=0.0,
                    op0=ALU.mult,
                    op1=ALU.add,
                )

        def quantise_h(g):
            h_codes[g] = work.tile([P, TOK], U32, align_bytes=64, tag="h_codes", bufs=3, name="h_codes%d" % g)
            h_scales[g] = work.tile([P, TOK], U8, align_bytes=64, tag="h_scales", bufs=3, name="h_scales%d" % g)
            nc.vector.quantize_mx(
                out=h_codes[g][:].bitcast(FP8X4),
                scales=h_scales[g][:],
                in_=h_grouped[g][:].rearrange("p c t -> p (c t)"),
            )

        def regroup_w1(j):
            w1_grouped[j] = const.tile([P, BANK, PACK], BF16, align_bytes=64, name="w1_grouped%d" % j)
            if W1_ON_G(j):
                dst, src = runs_of_four(w1_planes[j][:], w1_grouped[j][:])
                nc.gpsimd.tensor_scalar(out=dst, in0=src, scalar1=1.0, scalar2=0.0, op0=ALU.mult, op1=ALU.add)
            else:
                interleave(w1_planes[j], w1_grouped[j], BANK, S_W1)

        def quantise_w1(j):
            cols = slice(j * BANK, (j + 1) * BANK)
            nc.vector.quantize_mx(
                out=w1_codes[:, cols].bitcast(FP8X4),
                scales=w1_scales[:, cols],
                in_=w1_grouped[j][:].rearrange("p c t -> p (c t)"),
            )

        def stage2(i, half):
            g, s = divmod(i, GROUP)
            toks = slice(s * P, (s + 1) * P)
            act[i, half] = work.tile([P, HALF], F32, tag="act", bufs=12, name="act%d_%d" % (i, half))
            for j in range(HALF // BANK):
                cols = slice(half * HALF + j * BANK, half * HALF + (j + 1) * BANK)
                o_ps = psum.tile([P, BANK], F32, tag=TAG_O)
                nc.tensor.matmul_mx(
                    out=o_ps[:],
                    lhsT=h_codes[g][:, toks].bitcast(FP8X4),
                    lhsT_scale=h_scales[g][:, toks],
                    rhs=w1_codes[:, cols].bitcast(FP8X4),
                    rhs_scale=w1_scales[:, cols],
                    start=True,
                    stop=True,
                )
                nc.vector.tensor_tensor(
                    out=act[i, half][:, j * BANK : (j + 1) * BANK], in0=o_ps[:], in1=b1_bc[:, cols], op=ALU.add
                )

        def gelu_and_store(i, half, pieces=1):
            width = HALF // pieces
            for q in range(pieces):
                cols = slice(q * width, (q + 1) * width)
                nc.scalar.activation(out=act[i, half][:, cols], in_=act[i, half][:, cols], func=ACT.Gelu_apprx_tanh)
                nc.sync.dma_start(out=out[i][:, half * HALF + q * width : half * HALF + (q + 1) * width], in_=act[i, half][:, cols])

        posT_ps = psum.tile([P, P], BF16, tag=TAG_T)
        nc.tensor.transpose(posT_ps[:], pos_sb[:], ident_b[:])
        posT = const.tile([P, P], BF16)
        nc.vector.tensor_copy(out=posT[:], in_=posT_ps[:])
        gbT_ps = psum.tile([P, P], BF16, tag=TAG_Y)
        nc.tensor.transpose(gbT_ps[:], gb_rows[:], ident_b[:])
        gb = const.tile([P, 3 * PACK], F32)
        nc.vector.tensor_copy(out=gb[:], in_=gbT_ps[:, 0 : 3 * PACK])
        transpose_h2(0)
        empty_h2(0)
        if PRE_W1:
            regroup_w1(0)
        interleave(wx_planes, wx_grouped, D, S_WX)
        if HQ_FIRST:
            quantise_h2(0)
        nc.vector.quantize_mx(
            out=wx_codes[:].bitcast(FP8X4),
            scales=wx_scales[:],
            in_=wx_grouped[:].rearrange("p c t -> p (c t)"),
        )
        if not HQ_FIRST:
            quantise_h2(0)
        if PRE_W1:
            quantise_w1(0)

        H2_ODD = 0
        Q2_POS = 1
        MX_LAG = 1
        SQ_LAG = 2
        W1_STEP = 0
        W1_GAP = 1
        W1_LAG = 2
        NORM_LAG = 3
        NORM_POS = 1
        PLANE_LAG = 6
        OUT_LAG = 10
        GELU_LAG = 1
        w1_steps = [W1_STEP + j + (W1_GAP if 2 * j >= N_BLOCKS else 0) for j in range(N_BLOCKS)]
        for k in range(B + OUT_LAG + GELU_LAG):
            next_group = k // GROUP + 1
            if k < B:
                bias_part(k)
                plain_part(k)
                empty_t(k)
            if next_group < N_GROUPS and k % GROUP == H2_ODD:
                transpose_h2(next_group)
                empty_h2(next_group)
            if Q2_POS == 0 and next_group < N_GROUPS and k % GROUP == GROUP - 1:
                quantise_h2(next_group)
            if 0 <= k - MX_LAG < B:
                mx_part(k - MX_LAG)
                add_x1(k - MX_LAG)
            if Q2_POS == 1 and next_group < N_GROUPS and k % GROUP == GROUP - 1:
                quantise_h2(next_group)
            if 0 <= k - SQ_LAG < B:
                centred_squares(k - SQ_LAG)
                if (k - SQ_LAG) % GROUP == GROUP - 1:
                    normalise((k - SQ_LAG) // GROUP)
                    if not NORM_ON_V((k - SQ_LAG) // GROUP):
                        norm_rows((k - SQ_LAG) // GROUP)
            if NORM_POS == 0 and 0 <= k - NORM_LAG < B and (k - NORM_LAG) % GROUP == GROUP - 1 and NORM_ON_V((k - NORM_LAG) // GROUP):
                norm_rows((k - NORM_LAG) // GROUP)
            for j in range(N_BLOCKS):
                if k == w1_steps[j] and not (PRE_W1 and j == 0):
                    regroup_w1(j)
            if NORM_POS == 1 and 0 <= k - NORM_LAG < B and (k - NORM_LAG) % GROUP == GROUP - 1 and NORM_ON_V((k - NORM_LAG) // GROUP):
                norm_rows((k - NORM_LAG) // GROUP)
            if 0 <= k - PLANE_LAG < B:
                g, s = divmod(k - PLANE_LAG, GROUP)
                h_planes_bank(g, s * PLANES_A_BANK)
                empty_planes(g, s * PLANES_A_BANK)
                if s == GROUP - 1:
                    regroup_h(g)
            for j in range(N_BLOCKS):
                if k == w1_steps[j] + W1_LAG and not (PRE_W1 and j == 0):
                    quantise_w1(j)
            if 0 <= k - OUT_LAG + 1 < B and (k - OUT_LAG + 1) % GROUP == 0:
                quantise_h((k - OUT_LAG + 1) // GROUP)
            if 0 <= k - OUT_LAG < B:
                g, half = divmod(k - OUT_LAG, GROUP)
                for s in range(GROUP):
                    stage2(g * GROUP + s, half)
            if 0 <= k - OUT_LAG - GELU_LAG < B:
                g, half = divmod(k - OUT_LAG - GELU_LAG, GROUP)
                for s in range(GROUP):
                    gelu_and_store(g * GROUP + s, half)
            if NORM_POS == 2 and 0 <= k - NORM_LAG < B and (k - NORM_LAG) % GROUP == GROUP - 1 and NORM_ON_V((k - NORM_LAG) // GROUP):
                norm_rows((k - NORM_LAG) // GROUP)
